import numpy as np
import ml_dtypes


def mxq(x, axis, fmt="e4m3"):
    dtype, down = {"e4m3": (ml_dtypes.float8_e4m3fn, 7), "e5m2": (ml_dtypes.float8_e5m2, 14)}[fmt]
    v = np.moveaxis(np.asarray(x, np.float32).astype(ml_dtypes.bfloat16).astype(np.float64), axis, -1)
    blocks = v.reshape(v.shape[:-1] + (-1, 32))
    amax = np.abs(blocks).max(-1, keepdims=True)
    byte = np.maximum(np.where(amax > 0, np.frexp(amax)[1] - 1 + 127, 0) - down, 1)
    scale = np.exp2(byte - 127.0)
    codes = (blocks / scale).astype(np.float32).astype(dtype).astype(np.float64)
    return np.moveaxis((codes * scale).reshape(v.shape), -1, axis)


WIDE = False


def mx_kscale(k):
    if not WIDE:
        return np.ones(k)
    levels = np.array([10, -10, 5, -5, 0])
    a = np.random.permutation(np.resize(levels, k // 512 * 4)).reshape(k // 512, 4)
    idx = np.arange(k)
    return np.exp2(a[idx // 512, idx % 128 // 32])


BF16 = ml_dtypes.bfloat16


def bf(x):
    return np.asarray(x, np.float32).astype(BF16)


def f64(x):
    return np.asarray(x).astype(np.float64)


E2M1 = np.array([0.0, 0.5, 1.0, 1.5, 2.0, 3.0, 4.0, 6.0, -0.0, -0.5, -1.0, -1.5, -2.0, -3.0, -4.0, -6.0])


def pack_weight(w, fmt):
    k, n = w.shape
    w = f64(bf(w)).reshape(k // 32, 32, n)
    amax = np.abs(w).max(1)
    if fmt == "e4m3":
        byte = np.frexp(amax)[1] - 1 + 127 - 7
    else:
        mant, ex = np.frexp(amax / 6.0)
        byte = np.where(mant > 0.5, ex, ex - 1) + 127
    byte = np.clip(np.where(amax > 0, byte, 1), 1, 254)
    scaled = (w * np.exp2(127.0 - byte)[:, None, :]).reshape(k, n).astype(np.float32)
    by_word = np.ascontiguousarray(scaled.reshape(k // 512, 128, 4, n).transpose(0, 1, 3, 2))
    if fmt == "e4m3":
        words = by_word.astype(ml_dtypes.float8_e4m3fn).view(np.uint8)
    else:
        c = by_word.astype(ml_dtypes.float4_e2m1fn).view(np.uint8) & 0xF
        words = c[..., 0::2] | (c[..., 1::2] << 4)
    return np.ascontiguousarray(words), np.ascontiguousarray(byte.astype(np.uint8).reshape(k // 512, 16, n))


def unpack_weight(words, scales, fmt):
    g, p, n, _ = words.shape
    if fmt == "e4m3":
        vals = np.ascontiguousarray(words).view(ml_dtypes.float8_e4m3fn).astype(np.float64)
    else:
        nib = np.empty((g, p, n, 4), np.uint8)
        nib[..., 0::2] = words & 0xF
        nib[..., 1::2] = words >> 4
        vals = E2M1[nib]
    vals = vals * np.repeat(np.exp2(scales.astype(np.float64) - 127.0), 8, axis=1)[..., None]
    return vals.transpose(0, 1, 3, 2).reshape(g * 512, n)

def pack4(w):
    words, scales = pack_weight(w, "e2m1")
    return words.reshape(words.shape[0], 128, -1), scales


def unpack4(words, scales):
    return unpack_weight(words.reshape(words.shape[0], 128, -1, 2), scales, "e2m1")


H, D_CONTENT, D_POS, D_K, D_V, B, L = 8, 768, 256, 128, 128, 4, 256
D_MODEL = D_CONTENT + D_POS
T = B * L
DV1 = D_V // 2
KP = H * DV1
EPS = 1e-3


def setup_inputs():
    s1, s2 = mx_kscale(KP), mx_kscale(KP)
    sc = np.concatenate([s1.reshape(H, DV1), s2.reshape(H, DV1)], axis=1)
    attn_out = bf(np.random.standard_normal((H, B, L, D_V)) * 0.4 * sc[:, None, None, :])
    inp = bf(np.random.standard_normal((T, D_MODEL)) * 0.05 + np.random.standard_normal((T, 1)) * 0.03)
    w_proj1_words, w_proj1_scales = pack4(np.random.standard_normal((KP, D_CONTENT)) * 0.1 / np.sqrt(KP) / s1[:, None])
    w_proj2_words, w_proj2_scales = pack4(np.random.standard_normal((KP, D_POS)) * 0.1 / np.sqrt(KP) / s2[:, None])
    ln_a = bf(1.0 + 0.1 * np.random.standard_normal(D_MODEL))
    ln_b = bf(0.1 * np.random.standard_normal(D_MODEL))
    return {
        "attn_out": attn_out,
        "inp": inp,
        "w_proj1_words": w_proj1_words,
        "w_proj1_scales": w_proj1_scales,
        "w_proj2_words": w_proj2_words,
        "w_proj2_scales": w_proj2_scales,
        "ln_a": ln_a,
        "ln_b": ln_b,
    }


def reference(attn_out, inp, w_proj1_words, w_proj1_scales, w_proj2_words, w_proj2_scales, ln_a, ln_b):
    o = f64(attn_out).reshape(H, T, D_V).transpose(1, 0, 2)
    o1 = o[:, :, :DV1].reshape(T, KP)
    o2 = o[:, :, DV1:].reshape(T, KP)
    y1 = mxq(o1, 1, "e4m3") @ unpack4(w_proj1_words, w_proj1_scales)
    y2 = mxq(o2, 1, "e4m3") @ unpack4(w_proj2_words, w_proj2_scales)
    z = np.concatenate([y1, y2], -1) + f64(inp)
    mu = np.mean(z, axis=-1, keepdims=True)
    sigma = np.std(z, axis=-1, keepdims=True, ddof=1)
    ln = (z - mu) / (sigma + EPS)
    return ln * f64(ln_a) + f64(ln_b)

@@ -1,0 +1,309 @@
+from contextlib import ExitStack
+
+import concourse.mybir as mybir
+from concourse.masks import make_identity
+
+F32 = mybir.dt.float32
+BF16 = mybir.dt.bfloat16
+I32 = mybir.dt.int32
+U32 = mybir.dt.uint32
+U8 = mybir.dt.uint8
+FP8X4 = mybir.dt.float8_e4m3fn_x4
+FP4X4 = mybir.dt.float4_e2m1fn_x4
+ALU = mybir.AluOpType
+ACT = mybir.ActivationFunctionType
+
+P = 128
+PACK = 4
+HEADS = 8
+D_V = 128
+HALF = D_V // 2
+TOKENS = 1024
+D_MODEL = 1024
+D_CONTENT = 768
+N_TILES = TOKENS // P
+PASSES = HEADS * D_V // (P * PACK)
+HEADS_PER_PASS = HEADS // PASSES
+ROWS_PER_HALF = HALF // PACK
+BANK = 512
+BANKS_PER_ROW = D_MODEL // BANK
+EPS = 1e-3
+VECTOR_COLS = 512
+
+FLOPS = 2 * TOKENS * (HEADS * HALF) * D_MODEL
+
+
+def tile_multiheadattention_pa_kernel(
+    tc, attn_out, inp, w_proj1_words, w_proj1_scales, w_proj2_words, w_proj2_scales, ln_a, ln_b, out
+):
+    nc = tc.nc
+    with ExitStack() as stack:
+        const = stack.enter_context(tc.tile_pool(name="const", bufs=1))
+        loads = stack.enter_context(tc.tile_pool(name="loads", bufs=N_TILES))
+        stage = stack.enter_context(tc.tile_pool(name="stage", bufs=3))
+        rows = stack.enter_context(tc.tile_pool(name="rows", bufs=3))
+        results = stack.enter_context(tc.tile_pool(name="results", bufs=N_TILES))
+        stats = stack.enter_context(tc.tile_pool(name="stats", bufs=4))
+        xt_psum = stack.enter_context(tc.psum_pool(name="xt_psum", bufs=2))
+        z_psum = stack.enter_context(tc.psum_pool(name="z_psum", bufs=2))
+        ab_psum = stack.enter_context(tc.psum_pool(name="ab_psum", bufs=1))
+        stack.enter_context(tc.manual_schedule())
+
+        w_both = const.tile([P, PASSES, 2 * D_MODEL], U8, align_bytes=64)
+        w_scales = const.tile([P, PASSES, D_MODEL], U8, align_bytes=64)
+        ab_rows = const.tile([P, 2 * D_MODEL], BF16)
+        ones = const.tile([P, P], BF16)
+        one = const.tile([P, 1], F32)
+        nc.vector.memset(w_both[:].bitcast(I32), 0)
+        nc.vector.memset(w_scales[:].bitcast(I32), 0)
+        nc.vector.memset(ab_rows[:].bitcast(I32), 0)
+        nc.vector.memset(ones[:], 1.0)
+        nc.vector.memset(one[:], 1.0)
+
+        ident = const.tile([P, P], F32)
+        make_identity(nc, ident[:])
+        nc.gpsimd.dma_start(out=ab_rows[0:1, 0:D_MODEL], in_=ln_a.rearrange("(o n) -> o n", o=1))
+        nc.gpsimd.dma_start(out=ab_rows[0:1, D_MODEL : 2 * D_MODEL], in_=ln_b.rearrange("(o n) -> o n", o=1))
+
+        warm = const.tile([P, 1], F32)
+        nc.scalar.activation(out=warm[:], in_=one[:], func=ACT.Sqrt)
+
+        x_src = attn_out.rearrange("h b l f -> h (b l) f")
+        x_tiles = []
+        inp_tiles = []
+
+        def load_tile(i):
+            tokens = slice(P * i, P * (i + 1))
+            x_tile = loads.tile([P, HEADS, D_V], BF16)
+            nc.sync.dma_start(out=x_tile[:], in_=x_src[:, tokens, :].rearrange("h p f -> p h f"))
+            x_tiles.append(x_tile)
+            if i == 0:
+                load_weights()
+            inp_tile = loads.tile([P, D_MODEL], BF16)
+            nc.sync.dma_start(out=inp_tile[:], in_=inp[tokens, :])
+            inp_tiles.append(inp_tile)
+
+        def load_weights():
+            words_sb = w_both[:].bitcast(I32)
+            scales_sb = w_scales[:].bitcast(I32)
+            split_w = D_CONTENT // 2
+            split_s = D_CONTENT // 4
+            w1 = w_proj1_words[0].bitcast(I32).rearrange("(g h q) w -> h q g w", g=PASSES, h=HEADS_PER_PASS)
+            w2 = w_proj2_words[0].bitcast(I32).rearrange("(g h q) w -> h q g w", g=PASSES, h=HEADS_PER_PASS)
+            for h in range(HEADS_PER_PASS):
+                first = 2 * ROWS_PER_HALF * h
+                nc.sync.dma_start(out=words_sb[first : first + ROWS_PER_HALF, :, 0:split_w], in_=w1[h])
+                nc.sync.dma_start(
+                    out=words_sb[first + ROWS_PER_HALF : first + 2 * ROWS_PER_HALF, :, split_w:], in_=w2[h]
+                )
+            s1 = w_proj1_scales[0].bitcast(I32).rearrange("(g h e) w -> e h g w", g=PASSES, h=HEADS_PER_PASS)
+            s2 = w_proj2_scales[0].bitcast(I32).rearrange("(g h e) w -> e h g w", g=PASSES, h=HEADS_PER_PASS)
+            for e in range(2):
+                nc.sync.dma_start(out=scales_sb[e : P : 32, :, 0:split_s], in_=s1[e])
+                nc.sync.dma_start(out=scales_sb[2 + e : P : 32, :, split_s:], in_=s2[e])
+
+        for i in range(N_TILES):
+            load_tile(i)
+
+        grouped_tiles = {}
+        code_tiles = {}
+        z_banks = {}
+        z_rows = {}
+        o_rows = {}
+        small = {}
+
+        def transpose_tile(i):
+            x_words = x_tiles[i][:].rearrange("p h f -> p (h f)").bitcast(F32)
+            words_per_pass = P * PACK // 2
+            xt = xt_psum.tile([P, PASSES, 2, P], F32)
+            for g in range(PASSES):
+                for u in range(2):
+                    nc.tensor.transpose(
+                        xt[:, g, u, :],
+                        x_words[:, words_per_pass * g + u : words_per_pass * (g + 1) : 2],
+                        ident[:],
+                    )
+            grouped = stage.tile([P, PASSES, P, PACK], BF16, align_bytes=64)
+            grouped_words = (
+                grouped[:]
+                .rearrange("p g r t -> p (g r t)")
+                .bitcast(F32)
+                .rearrange("p (g r u) -> p g r u", g=PASSES, u=2)
+            )
+            nc.scalar.copy(out=grouped_words, in_=xt[:].rearrange("p g u r -> p g r u"))
+            grouped_tiles[i] = grouped
+
+        def quantise_tile(i):
+            codes = stage.tile([P, PASSES * P], U32, align_bytes=64)
+            code_scales = stage.tile([P, PASSES * P], U8, align_bytes=64)
+            nc.vector.quantize_mx(
+                out=codes[:].bitcast(FP8X4),
+                scales=code_scales[:],
+                in_=grouped_tiles[i][:].rearrange("p g r t -> p (g r t)"),
+            )
+            code_tiles[i] = (codes, code_scales)
+
+        def project_tile(i):
+            codes, code_scales = code_tiles[i]
+            z = z_psum.tile([P, BANKS_PER_ROW, BANK], F32)
+            for c in range(BANKS_PER_ROW):
+                for g in range(PASSES):
+                    nc.tensor.matmul_mx(
+                        out=z[:, c, :],
+                        lhsT=codes[:, P * g : P * (g + 1)].bitcast(FP8X4),
+                        lhsT_scale=code_scales[:, P * g : P * (g + 1)],
+                        rhs=w_both[:, g, 2 * BANK * c : 2 * BANK * (c + 1)].bitcast(FP4X4),
+                        rhs_scale=w_scales[:, g, BANK * c : BANK * (c + 1)],
+                        start=(g == 0),
+                        stop=(g == PASSES - 1),
+                    )
+            z_banks[i] = z
+
+        def add_residual(i, c):
+            if c == 0:
+                z_row = rows.tile([P, D_MODEL], F32)
+                sums = stats.tile([P, BANKS_PER_ROW], F32)
+                z_rows[i] = z_row
+                small[i] = {"sums": sums}
+            cols = slice(BANK * c, BANK * (c + 1))
+            nc.vector.scalar_tensor_tensor(
+                out=z_rows[i][:, cols],
+                in0=z_banks[i][:, c, :],
+                scalar=1.0,
+                in1=inp_tiles[i][:, cols],
+                op0=ALU.mult,
+                op1=ALU.add,
+                accum_out=small[i]["sums"][:, c : c + 1],
+            )
+
+        def negative_mean(i):
+            neg_mean = stats.tile([P, 1], F32)
+            sums = small[i]["sums"]
+            nc.vector.tensor_scalar(
+                out=neg_mean[:],
+                in0=sums[:, 0:1],
+                scalar1=sums[:, 1:2],
+                scalar2=-1.0 / D_MODEL,
+                op0=ALU.add,
+                op1=ALU.mult,
+            )
+            small[i]["neg_mean"] = neg_mean
+
+        def sum_of_squares(i):
+            squares = rows.tile([P, D_MODEL], BF16)
+            ssq = stats.tile([P, 1], F32)
+            nc.scalar.activation(
+                out=squares[:], in_=z_rows[i][:], func=ACT.Square, bias=small[i]["neg_mean"][:], accum_out=ssq[:]
+            )
+            small[i]["ssq"] = ssq
+
+        def deviation(i):
+            sigma = stats.tile([P, 1], F32)
+            nc.scalar.activation(out=sigma[:], in_=small[i]["ssq"][:], func=ACT.Sqrt, scale=1.0 / (D_MODEL - 1))
+            small[i]["sigma"] = sigma
+
+        def add_eps(i):
+            sigma_eps = stats.tile([P, 1], F32)
+            nc.vector.tensor_scalar_add(out=sigma_eps[:], in0=small[i]["sigma"][:], scalar1=EPS)
+            small[i]["sigma_eps"] = sigma_eps
+
+        def invert(i):
+            rstd = stats.tile([P, 1], F32)
+            nc.vector.reciprocal(out=rstd[:], in_=small[i]["sigma_eps"][:])
+            small[i]["rstd"] = rstd
+
+        def shift_over_sigma(i):
+            neg_mean_rstd = stats.tile([P, 1], F32)
+            nc.vector.tensor_mul(out=neg_mean_rstd[:], in0=small[i]["neg_mean"][:], in1=small[i]["rstd"][:])
+            small[i]["neg_mean_rstd"] = neg_mean_rstd
+
+        def vector_gain(i):
+            o_row = results.tile([P, D_MODEL], F32)
+            o_rows[i] = o_row
+            nc.vector.scalar_tensor_tensor(
+                out=o_row[:, 0:VECTOR_COLS],
+                in0=z_rows[i][:, 0:VECTOR_COLS],
+                scalar=small[i]["neg_mean"][:],
+                in1=ab_low[:, 0, 0:VECTOR_COLS],
+                op0=ALU.add,
+                op1=ALU.mult,
+            )
+
+        def vector_bias(i):
+            nc.vector.scalar_tensor_tensor(
+                out=o_rows[i][:, 0:VECTOR_COLS],
+                in0=o_rows[i][:, 0:VECTOR_COLS],
+                scalar=small[i]["rstd"][:],
+                in1=ab_low[:, 1, 0:VECTOR_COLS],
+                op0=ALU.mult,
+                op1=ALU.add,
+            )
+
+        def scalar_normalise(i):
+            nc.scalar.activation(
+                out=o_rows[i][:, VECTOR_COLS:],
+                in_=z_rows[i][:, VECTOR_COLS:],
+                func=ACT.Identity,
+                bias=small[i]["neg_mean_rstd"][:],
+                scale=small[i]["rstd"][:],
+            )
+
+        def gpsimd_gain_bias(i):
+            rest = o_rows[i][:, VECTOR_COLS:]
+            nc.gpsimd.tensor_tensor(out=rest, in0=rest, in1=ab_high[:, 0, :], op=ALU.mult)
+            nc.gpsimd.tensor_tensor(out=rest, in0=rest, in1=ab_high[:, 1, :], op=ALU.add)
+
+        def store_tile(i):
+            nc.sync.dma_start(out=out[P * i : P * (i + 1), :], in_=o_rows[i][:])
+
+        transpose_tile(0)
+        quantise_tile(0)
+        ab_low = ab_psum.tile([P, 2, BANK], F32)
+        ab_rest = z_psum.tile([P, 2, BANK], F32, tag="z")
+        ab_high = const.tile([P, 2, D_MODEL - VECTOR_COLS], F32)
+        for v in range(2):
+            nc.tensor.matmul(
+                ab_low[:, v, :], lhsT=ones[:], rhs=ab_rows[:, D_MODEL * v : D_MODEL * v + BANK], start=True, stop=True
+            )
+            nc.tensor.matmul(
+                ab_rest[:, v, :],
+                lhsT=ones[:],
+                rhs=ab_rows[:, D_MODEL * v + BANK : D_MODEL * (v + 1)],
+                start=True,
+                stop=True,
+            )
+            nc.scalar.copy(out=ab_high[:, v, :], in_=ab_rest[:, v, :])
+        project_tile(0)
+        transpose_tile(1)
+
+        for i in range(N_TILES + 1):
+            now = i < N_TILES
+            before = i >= 1
+            if now:
+                add_residual(i, 0)
+            if before:
+                add_eps(i - 1)
+            if now:
+                add_residual(i, 1)
+            if before:
+                invert(i - 1)
+            if now:
+                negative_mean(i)
+            if i + 1 < N_TILES:
+                quantise_tile(i + 1)
+                project_tile(i + 1)
+            if before:
+                shift_over_sigma(i - 1)
+                vector_bias(i - 1)
+            if now:
+                vector_gain(i)
+                sum_of_squares(i)
+            if before:
+                scalar_normalise(i - 1)
+            if now:
+                deviation(i)
+            if i + 2 < N_TILES:
+                transpose_tile(i + 2)
+            if before:
+                gpsimd_gain_bias(i - 1)
+                store_tile(i - 1)

@@ -56,14 +56,14 @@ def tile_multiheadattention_pa_kernel(
         one = const.tile([P, 1], F32)
         nc.vector.memset(w_both[:].bitcast(I32), 0)
         nc.vector.memset(w_scales[:].bitcast(I32), 0)
-        nc.vector.memset(ab_rows[:].bitcast(I32), 0)
         nc.vector.memset(ones[:], 1.0)
         nc.vector.memset(one[:], 1.0)
 
+        nc.gpsimd.memset(ab_rows[:].bitcast(F32), 0.0)
+        nc.scalar.dma_start(out=ab_rows[0:1, 0:D_MODEL], in_=ln_a.rearrange("(o n) -> o n", o=1))
+        nc.scalar.dma_start(out=ab_rows[0:1, D_MODEL : 2 * D_MODEL], in_=ln_b.rearrange("(o n) -> o n", o=1))
         ident = const.tile([P, P], F32)
         make_identity(nc, ident[:])
-        nc.gpsimd.dma_start(out=ab_rows[0:1, 0:D_MODEL], in_=ln_a.rearrange("(o n) -> o n", o=1))
-        nc.gpsimd.dma_start(out=ab_rows[0:1, D_MODEL : 2 * D_MODEL], in_=ln_b.rearrange("(o n) -> o n", o=1))
 
         warm = const.tile([P, 1], F32)
         nc.scalar.activation(out=warm[:], in_=one[:], func=ACT.Sqrt)
@@ -217,7 +217,7 @@ def tile_multiheadattention_pa_kernel(
             nc.vector.tensor_mul(out=neg_mean_rstd[:], in0=small[i]["neg_mean"][:], in1=small[i]["rstd"][:])
             small[i]["neg_mean_rstd"] = neg_mean_rstd
 
-        def vector_gain(i):
+        def vector_gain(i, whole_row):
             o_row = results.tile([P, D_MODEL], F32)
             o_rows[i] = o_row
             nc.vector.scalar_tensor_tensor(
@@ -228,8 +228,17 @@ def tile_multiheadattention_pa_kernel(
                 op0=ALU.add,
                 op1=ALU.mult,
             )
+            if whole_row:
+                nc.vector.scalar_tensor_tensor(
+                    out=o_row[:, VECTOR_COLS:],
+                    in0=z_rows[i][:, VECTOR_COLS:],
+                    scalar=small[i]["neg_mean"][:],
+                    in1=ab_high[:, 0, :],
+                    op0=ALU.add,
+                    op1=ALU.mult,
+                )
 
-        def vector_bias(i):
+        def vector_bias(i, whole_row):
             nc.vector.scalar_tensor_tensor(
                 out=o_rows[i][:, 0:VECTOR_COLS],
                 in0=o_rows[i][:, 0:VECTOR_COLS],
@@ -238,6 +247,15 @@ def tile_multiheadattention_pa_kernel(
                 op0=ALU.mult,
                 op1=ALU.add,
             )
+            if whole_row:
+                nc.vector.scalar_tensor_tensor(
+                    out=o_rows[i][:, VECTOR_COLS:],
+                    in0=o_rows[i][:, VECTOR_COLS:],
+                    scalar=small[i]["rstd"][:],
+                    in1=ab_high[:, 1, :],
+                    op0=ALU.mult,
+                    op1=ALU.add,
+                )
 
         def scalar_normalise(i):
             nc.scalar.activation(
@@ -276,34 +294,34 @@ def tile_multiheadattention_pa_kernel(
         project_tile(0)
         transpose_tile(1)
 
+        last = N_TILES - 1
         for i in range(N_TILES + 1):
             now = i < N_TILES
             before = i >= 1
             if now:
                 add_residual(i, 0)
+                add_residual(i, 1)
+                negative_mean(i)
             if before:
                 add_eps(i - 1)
-            if now:
-                add_residual(i, 1)
-            if before:
-                invert(i - 1)
-            if now:
-                negative_mean(i)
             if i + 1 < N_TILES:
                 quantise_tile(i + 1)
                 project_tile(i + 1)
             if before:
-                shift_over_sigma(i - 1)
-                vector_bias(i - 1)
+                invert(i - 1)
             if now:
-                vector_gain(i)
+                vector_gain(i, i == last)
                 sum_of_squares(i)
-            if before:
+            if before and i - 1 != last:
+                shift_over_sigma(i - 1)
                 scalar_normalise(i - 1)
+            if before:
+                vector_bias(i - 1, i - 1 == last)
             if now:
                 deviation(i)
             if i + 2 < N_TILES:
                 transpose_tile(i + 2)
-            if before:
+            if before and i - 1 != last:
                 gpsimd_gain_bias(i - 1)
+            if before:
                 store_tile(i - 1)

@@ -30,6 +30,8 @@ BANKS_PER_ROW = D_MODEL // BANK
 EPS = 1e-3
 VECTOR_COLS = 512
 
+GPSIMD_HELPS = False
+
 FLOPS = 2 * TOKENS * (HEADS * HALF) * D_MODEL
 
 
@@ -294,7 +296,6 @@ def tile_multiheadattention_pa_kernel(
         project_tile(0)
         transpose_tile(1)
 
-        last = N_TILES - 1
         for i in range(N_TILES + 1):
             now = i < N_TILES
             before = i >= 1
@@ -310,18 +311,18 @@ def tile_multiheadattention_pa_kernel(
             if before:
                 invert(i - 1)
             if now:
-                vector_gain(i, i == last)
+                vector_gain(i, True)
                 sum_of_squares(i)
-            if before and i - 1 != last:
+            if before and GPSIMD_HELPS:
                 shift_over_sigma(i - 1)
                 scalar_normalise(i - 1)
             if before:
-                vector_bias(i - 1, i - 1 == last)
+                vector_bias(i - 1, True)
             if now:
                 deviation(i)
             if i + 2 < N_TILES:
                 transpose_tile(i + 2)
-            if before and i - 1 != last:
+            if before and GPSIMD_HELPS:
                 gpsimd_gain_bias(i - 1)
             if before:
                 store_tile(i - 1)

@@ -28,9 +28,6 @@ ROWS_PER_HALF = HALF // PACK
 BANK = 512
 BANKS_PER_ROW = D_MODEL // BANK
 EPS = 1e-3
-VECTOR_COLS = 512
-
-GPSIMD_HELPS = False
 
 FLOPS = 2 * TOKENS * (HEADS * HALF) * D_MODEL
 
@@ -47,8 +44,7 @@ def tile_multiheadattention_pa_kernel(
         results = stack.enter_context(tc.tile_pool(name="results", bufs=N_TILES))
         stats = stack.enter_context(tc.tile_pool(name="stats", bufs=4))
         xt_psum = stack.enter_context(tc.psum_pool(name="xt_psum", bufs=2))
-        z_psum = stack.enter_context(tc.psum_pool(name="z_psum", bufs=2))
-        ab_psum = stack.enter_context(tc.psum_pool(name="ab_psum", bufs=1))
+        z_psum = stack.enter_context(tc.psum_pool(name="z_psum", bufs=3))
         stack.enter_context(tc.manual_schedule())
 
         w_both = const.tile([P, PASSES, 2 * D_MODEL], U8, align_bytes=64)
@@ -74,15 +70,14 @@ def tile_multiheadattention_pa_kernel(
         x_tiles = []
         inp_tiles = []
 
-        def load_tile(i):
-            tokens = slice(P * i, P * (i + 1))
+        def load_x(i):
             x_tile = loads.tile([P, HEADS, D_V], BF16)
-            nc.sync.dma_start(out=x_tile[:], in_=x_src[:, tokens, :].rearrange("h p f -> p h f"))
+            nc.sync.dma_start(out=x_tile[:], in_=x_src[:, P * i : P * (i + 1), :].rearrange("h p f -> p h f"))
             x_tiles.append(x_tile)
-            if i == 0:
-                load_weights()
+
+        def load_inp(i):
             inp_tile = loads.tile([P, D_MODEL], BF16)
-            nc.sync.dma_start(out=inp_tile[:], in_=inp[tokens, :])
+            nc.sync.dma_start(out=inp_tile[:], in_=inp[P * i : P * (i + 1), :])
             inp_tiles.append(inp_tile)
 
         def load_weights():
@@ -104,9 +99,14 @@ def tile_multiheadattention_pa_kernel(
                 nc.sync.dma_start(out=scales_sb[e : P : 32, :, 0:split_s], in_=s1[e])
                 nc.sync.dma_start(out=scales_sb[2 + e : P : 32, :, split_s:], in_=s2[e])
 
+        load_x(0)
+        load_weights()
         for i in range(N_TILES):
-            load_tile(i)
+            if i + 1 < N_TILES:
+                load_x(i + 1)
+            load_inp(i)
 
+        xt_banks = {}
         grouped_tiles = {}
         code_tiles = {}
         z_banks = {}
@@ -114,7 +114,7 @@ def tile_multiheadattention_pa_kernel(
         o_rows = {}
         small = {}
 
-        def transpose_tile(i):
+        def transpose_only(i):
             x_words = x_tiles[i][:].rearrange("p h f -> p (h f)").bitcast(F32)
             words_per_pass = P * PACK // 2
             xt = xt_psum.tile([P, PASSES, 2, P], F32)
@@ -125,6 +125,10 @@ def tile_multiheadattention_pa_kernel(
                         x_words[:, words_per_pass * g + u : words_per_pass * (g + 1) : 2],
                         ident[:],
                     )
+            xt_banks[i] = xt
+
+        def copy_out(i):
+            xt = xt_banks[i]
             grouped = stage.tile([P, PASSES, P, PACK], BF16, align_bytes=64)
             grouped_words = (
                 grouped[:]
@@ -134,6 +138,10 @@ def tile_multiheadattention_pa_kernel(
             )
             nc.scalar.copy(out=grouped_words, in_=xt[:].rearrange("p g u r -> p g r u"))
             grouped_tiles[i] = grouped
+
+        def transpose_tile(i):
+            transpose_only(i)
+            copy_out(i)
 
         def quantise_tile(i):
             codes = stage.tile([P, PASSES * P], U32, align_bytes=64)
@@ -179,15 +187,10 @@ def tile_multiheadattention_pa_kernel(
             )
 
         def negative_mean(i):
+            scaled = stats.tile([P, BANKS_PER_ROW], F32)
             neg_mean = stats.tile([P, 1], F32)
-            sums = small[i]["sums"]
-            nc.vector.tensor_scalar(
-                out=neg_mean[:],
-                in0=sums[:, 0:1],
-                scalar1=sums[:, 1:2],
-                scalar2=-1.0 / D_MODEL,
-                op0=ALU.add,
-                op1=ALU.mult,
+            nc.scalar.activation(
+                out=scaled[:], in_=small[i]["sums"][:], func=ACT.Identity, scale=-1.0 / D_MODEL, accum_out=neg_mean[:]
             )
             small[i]["neg_mean"] = neg_mean
 
@@ -214,115 +217,67 @@ def tile_multiheadattention_pa_kernel(
             nc.vector.reciprocal(out=rstd[:], in_=small[i]["sigma_eps"][:])
             small[i]["rstd"] = rstd
 
-        def shift_over_sigma(i):
-            neg_mean_rstd = stats.tile([P, 1], F32)
-            nc.vector.tensor_mul(out=neg_mean_rstd[:], in0=small[i]["neg_mean"][:], in1=small[i]["rstd"][:])
-            small[i]["neg_mean_rstd"] = neg_mean_rstd
-
-        def vector_gain(i, whole_row):
+        def vector_gain(i):
             o_row = results.tile([P, D_MODEL], F32)
             o_rows[i] = o_row
             nc.vector.scalar_tensor_tensor(
-                out=o_row[:, 0:VECTOR_COLS],
-                in0=z_rows[i][:, 0:VECTOR_COLS],
+                out=o_row[:],
+                in0=z_rows[i][:],
                 scalar=small[i]["neg_mean"][:],
-                in1=ab_low[:, 0, 0:VECTOR_COLS],
+                in1=gain_bias[:, 0, :],
                 op0=ALU.add,
                 op1=ALU.mult,
             )
-            if whole_row:
-                nc.vector.scalar_tensor_tensor(
-                    out=o_row[:, VECTOR_COLS:],
-                    in0=z_rows[i][:, VECTOR_COLS:],
-                    scalar=small[i]["neg_mean"][:],
-                    in1=ab_high[:, 0, :],
-                    op0=ALU.add,
-                    op1=ALU.mult,
-                )
 
-        def vector_bias(i, whole_row):
+        def vector_bias(i):
             nc.vector.scalar_tensor_tensor(
-                out=o_rows[i][:, 0:VECTOR_COLS],
-                in0=o_rows[i][:, 0:VECTOR_COLS],
+                out=o_rows[i][:],
+                in0=o_rows[i][:],
                 scalar=small[i]["rstd"][:],
-                in1=ab_low[:, 1, 0:VECTOR_COLS],
+                in1=gain_bias[:, 1, :],
                 op0=ALU.mult,
                 op1=ALU.add,
             )
-            if whole_row:
-                nc.vector.scalar_tensor_tensor(
-                    out=o_rows[i][:, VECTOR_COLS:],
-                    in0=o_rows[i][:, VECTOR_COLS:],
-                    scalar=small[i]["rstd"][:],
-                    in1=ab_high[:, 1, :],
-                    op0=ALU.mult,
-                    op1=ALU.add,
-                )
-
-        def scalar_normalise(i):
-            nc.scalar.activation(
-                out=o_rows[i][:, VECTOR_COLS:],
-                in_=z_rows[i][:, VECTOR_COLS:],
-                func=ACT.Identity,
-                bias=small[i]["neg_mean_rstd"][:],
-                scale=small[i]["rstd"][:],
-            )
-
-        def gpsimd_gain_bias(i):
-            rest = o_rows[i][:, VECTOR_COLS:]
-            nc.gpsimd.tensor_tensor(out=rest, in0=rest, in1=ab_high[:, 0, :], op=ALU.mult)
-            nc.gpsimd.tensor_tensor(out=rest, in0=rest, in1=ab_high[:, 1, :], op=ALU.add)
 
         def store_tile(i):
             nc.sync.dma_start(out=out[P * i : P * (i + 1), :], in_=o_rows[i][:])
 
         transpose_tile(0)
         quantise_tile(0)
-        ab_low = ab_psum.tile([P, 2, BANK], F32)
-        ab_rest = z_psum.tile([P, 2, BANK], F32, tag="z")
-        ab_high = const.tile([P, 2, D_MODEL - VECTOR_COLS], F32)
+        gain_bias = const.tile([P, 2, D_MODEL], F32)
         for v in range(2):
-            nc.tensor.matmul(
-                ab_low[:, v, :], lhsT=ones[:], rhs=ab_rows[:, D_MODEL * v : D_MODEL * v + BANK], start=True, stop=True
-            )
-            nc.tensor.matmul(
-                ab_rest[:, v, :],
-                lhsT=ones[:],
-                rhs=ab_rows[:, D_MODEL * v + BANK : D_MODEL * (v + 1)],
-                start=True,
-                stop=True,
-            )
-            nc.scalar.copy(out=ab_high[:, v, :], in_=ab_rest[:, v, :])
+            spread = z_psum.tile([P, BANKS_PER_ROW, BANK], F32, tag="z")
+            for c in range(BANKS_PER_ROW):
+                first = D_MODEL * v + BANK * c
+                nc.tensor.matmul(spread[:, c, :], lhsT=ones[:], rhs=ab_rows[:, first : first + BANK], start=True, stop=True)
+                nc.scalar.copy(out=gain_bias[:, v, BANK * c : BANK * (c + 1)], in_=spread[:, c, :])
         project_tile(0)
         transpose_tile(1)
+        transpose_only(2)
 
         for i in range(N_TILES + 1):
             now = i < N_TILES
             before = i >= 1
             if now:
                 add_residual(i, 0)
+            if before:
+                add_eps(i - 1)
+            if now:
                 add_residual(i, 1)
                 negative_mean(i)
             if before:
-                add_eps(i - 1)
+                invert(i - 1)
             if i + 1 < N_TILES:
                 quantise_tile(i + 1)
                 project_tile(i + 1)
+            if i + 3 < N_TILES:
+                transpose_only(i + 3)
             if before:
-                invert(i - 1)
+                vector_bias(i - 1)
+                store_tile(i - 1)
             if now:
-                vector_gain(i, True)
+                vector_gain(i)
                 sum_of_squares(i)
-            if before and GPSIMD_HELPS:
-                shift_over_sigma(i - 1)
-                scalar_normalise(i - 1)
-            if before:
-                vector_bias(i - 1, True)
-            if now:
                 deviation(i)
             if i + 2 < N_TILES:
-                transpose_tile(i + 2)
-            if before and GPSIMD_HELPS:
-                gpsimd_gain_bias(i - 1)
-            if before:
-                store_tile(i - 1)
+                copy_out(i + 2)

@@ -28,6 +28,7 @@ ROWS_PER_HALF = HALF // PACK
 BANK = 512
 BANKS_PER_ROW = D_MODEL // BANK
 EPS = 1e-3
+VECTOR_COLS = 704
 
 FLOPS = 2 * TOKENS * (HEADS * HALF) * D_MODEL
 
@@ -44,7 +45,8 @@ def tile_multiheadattention_pa_kernel(
         results = stack.enter_context(tc.tile_pool(name="results", bufs=N_TILES))
         stats = stack.enter_context(tc.tile_pool(name="stats", bufs=4))
         xt_psum = stack.enter_context(tc.psum_pool(name="xt_psum", bufs=2))
-        z_psum = stack.enter_context(tc.psum_pool(name="z_psum", bufs=3))
+        z_psum = stack.enter_context(tc.psum_pool(name="z_psum", bufs=1))
+        ab_psum = stack.enter_context(tc.psum_pool(name="ab_psum", bufs=1))
         stack.enter_context(tc.manual_schedule())
 
         w_both = const.tile([P, PASSES, 2 * D_MODEL], U8, align_bytes=64)
@@ -56,6 +58,8 @@ def tile_multiheadattention_pa_kernel(
         nc.vector.memset(w_scales[:].bitcast(I32), 0)
         nc.vector.memset(ones[:], 1.0)
         nc.vector.memset(one[:], 1.0)
+        minus_one = const.tile([P, 1], F32)
+        nc.vector.memset(minus_one[:], -1.0)
 
         nc.gpsimd.memset(ab_rows[:].bitcast(F32), 0.0)
         nc.scalar.dma_start(out=ab_rows[0:1, 0:D_MODEL], in_=ln_a.rearrange("(o n) -> o n", o=1))
@@ -207,77 +211,96 @@ def tile_multiheadattention_pa_kernel(
             nc.scalar.activation(out=sigma[:], in_=small[i]["ssq"][:], func=ACT.Sqrt, scale=1.0 / (D_MODEL - 1))
             small[i]["sigma"] = sigma
 
-        def add_eps(i):
+        def inverse_deviation(i):
             sigma_eps = stats.tile([P, 1], F32)
-            nc.vector.tensor_scalar_add(out=sigma_eps[:], in0=small[i]["sigma"][:], scalar1=EPS)
-            small[i]["sigma_eps"] = sigma_eps
-
-        def invert(i):
             rstd = stats.tile([P, 1], F32)
-            nc.vector.reciprocal(out=rstd[:], in_=small[i]["sigma_eps"][:])
+            nc.gpsimd.tensor_scalar_add(out=sigma_eps[:], in0=small[i]["sigma"][:], scalar1=EPS)
+            nc.gpsimd.tensor_tensor(out=rstd[:], in0=sigma_eps[:], in1=minus_one[:], op=ALU.pow)
             small[i]["rstd"] = rstd
 
-        def vector_gain(i):
+        def vector_pieces(whole_row):
+            end = D_MODEL if whole_row else VECTOR_COLS
+            return [(0, 0, BANK), (1, BANK, end - BANK)]
+
+        def vector_gain(i, whole_row):
             o_row = results.tile([P, D_MODEL], F32)
             o_rows[i] = o_row
-            nc.vector.scalar_tensor_tensor(
-                out=o_row[:],
-                in0=z_rows[i][:],
-                scalar=small[i]["neg_mean"][:],
-                in1=gain_bias[:, 0, :],
+            for c, first, width in vector_pieces(whole_row):
+                nc.vector.scalar_tensor_tensor(
+                    out=o_row[:, first : first + width],
+                    in0=z_rows[i][:, first : first + width],
+                    scalar=small[i]["neg_mean"][:],
+                    in1=gain_bias[:, 0, c, 0:width],
+                    op0=ALU.add,
+                    op1=ALU.mult,
+                )
+
+        def vector_bias(i, whole_row):
+            for c, first, width in vector_pieces(whole_row):
+                nc.vector.scalar_tensor_tensor(
+                    out=o_rows[i][:, first : first + width],
+                    in0=o_rows[i][:, first : first + width],
+                    scalar=small[i]["rstd"][:],
+                    in1=gain_bias[:, 1, c, 0:width],
+                    op0=ALU.mult,
+                    op1=ALU.add,
+                )
+
+        def gpsimd_rest(i):
+            rest = o_rows[i][:, VECTOR_COLS:]
+            nc.gpsimd.tensor_scalar(
+                out=rest,
+                in0=z_rows[i][:, VECTOR_COLS:],
+                scalar1=small[i]["neg_mean"][:],
+                scalar2=small[i]["rstd"][:],
                 op0=ALU.add,
                 op1=ALU.mult,
             )
-
-        def vector_bias(i):
-            nc.vector.scalar_tensor_tensor(
-                out=o_rows[i][:],
-                in0=o_rows[i][:],
-                scalar=small[i]["rstd"][:],
-                in1=gain_bias[:, 1, :],
-                op0=ALU.mult,
-                op1=ALU.add,
-            )
+            nc.gpsimd.tensor_tensor(out=rest, in0=rest, in1=ab_high[:, 0, :], op=ALU.mult)
+            nc.gpsimd.tensor_tensor(out=rest, in0=rest, in1=ab_high[:, 1, :], op=ALU.add)
 
         def store_tile(i):
             nc.sync.dma_start(out=out[P * i : P * (i + 1), :], in_=o_rows[i][:])
 
         transpose_tile(0)
         quantise_tile(0)
-        gain_bias = const.tile([P, 2, D_MODEL], F32)
+        gain_bias = ab_psum.tile([P, 2, BANKS_PER_ROW, BANK], F32)
+        ab_high = const.tile([P, 2, D_MODEL - VECTOR_COLS], F32)
         for v in range(2):
-            spread = z_psum.tile([P, BANKS_PER_ROW, BANK], F32, tag="z")
             for c in range(BANKS_PER_ROW):
                 first = D_MODEL * v + BANK * c
-                nc.tensor.matmul(spread[:, c, :], lhsT=ones[:], rhs=ab_rows[:, first : first + BANK], start=True, stop=True)
-                nc.scalar.copy(out=gain_bias[:, v, BANK * c : BANK * (c + 1)], in_=spread[:, c, :])
+                nc.tensor.matmul(
+                    gain_bias[:, v, c, :], lhsT=ones[:], rhs=ab_rows[:, first : first + BANK], start=True, stop=True
+                )
+            nc.scalar.copy(out=ab_high[:, v, :], in_=gain_bias[:, v, 1, VECTOR_COLS - BANK :])
         project_tile(0)
         transpose_tile(1)
-        transpose_only(2)
+        transpose_tile(2)
 
+        last = N_TILES - 1
         for i in range(N_TILES + 1):
             now = i < N_TILES
             before = i >= 1
-            if now:
-                add_residual(i, 0)
-            if before:
-                add_eps(i - 1)
-            if now:
-                add_residual(i, 1)
-                negative_mean(i)
-            if before:
-                invert(i - 1)
             if i + 1 < N_TILES:
                 quantise_tile(i + 1)
+            if now:
+                add_residual(i, 0)
+                add_residual(i, 1)
+                negative_mean(i)
+            if i + 1 < N_TILES:
                 project_tile(i + 1)
             if i + 3 < N_TILES:
                 transpose_only(i + 3)
             if before:
-                vector_bias(i - 1)
+                inverse_deviation(i - 1)
+                vector_bias(i - 1, i - 1 == last)
+            if before and i - 1 != last:
+                gpsimd_rest(i - 1)
+            if before:
                 store_tile(i - 1)
             if now:
-                vector_gain(i)
+                vector_gain(i, i == last)
                 sum_of_squares(i)
                 deviation(i)
-            if i + 2 < N_TILES:
-                copy_out(i + 2)
+            if i + 3 < N_TILES:
+                copy_out(i + 3)

@@ -28,6 +28,7 @@ ROWS_PER_HALF = HALF // PACK
 BANK = 512
 BANKS_PER_ROW = D_MODEL // BANK
 EPS = 1e-3
+TINY = 1e-30
 VECTOR_COLS = 704
 
 FLOPS = 2 * TOKENS * (HEADS * HALF) * D_MODEL
@@ -58,8 +59,6 @@ def tile_multiheadattention_pa_kernel(
         nc.vector.memset(w_scales[:].bitcast(I32), 0)
         nc.vector.memset(ones[:], 1.0)
         nc.vector.memset(one[:], 1.0)
-        minus_one = const.tile([P, 1], F32)
-        nc.vector.memset(minus_one[:], -1.0)
 
         nc.gpsimd.memset(ab_rows[:].bitcast(F32), 0.0)
         nc.scalar.dma_start(out=ab_rows[0:1, 0:D_MODEL], in_=ln_a.rearrange("(o n) -> o n", o=1))
@@ -68,7 +67,7 @@ def tile_multiheadattention_pa_kernel(
         make_identity(nc, ident[:])
 
         warm = const.tile([P, 1], F32)
-        nc.scalar.activation(out=warm[:], in_=one[:], func=ACT.Sqrt)
+        nc.scalar.activation(out=warm[:], in_=one[:], func=ACT.Abs_reciprocal_sqrt)
 
         x_src = attn_out.rearrange("h b l f -> h (b l) f")
         x_tiles = []
@@ -207,15 +206,19 @@ def tile_multiheadattention_pa_kernel(
             small[i]["ssq"] = ssq
 
         def deviation(i):
-            sigma = stats.tile([P, 1], F32)
-            nc.scalar.activation(out=sigma[:], in_=small[i]["ssq"][:], func=ACT.Sqrt, scale=1.0 / (D_MODEL - 1))
-            small[i]["sigma"] = sigma
-
-        def inverse_deviation(i):
-            sigma_eps = stats.tile([P, 1], F32)
+            ssq = small[i]["ssq"]
+            inv_sigma = stats.tile([P, 1], F32)
+            sigma_n = stats.tile([P, 1], F32)
+            shifted_sq = stats.tile([P, 1], F32)
             rstd = stats.tile([P, 1], F32)
-            nc.gpsimd.tensor_scalar_add(out=sigma_eps[:], in0=small[i]["sigma"][:], scalar1=EPS)
-            nc.gpsimd.tensor_tensor(out=rstd[:], in0=sigma_eps[:], in1=minus_one[:], op=ALU.pow)
+            nc.scalar.activation(
+                out=inv_sigma[:], in_=ssq[:], func=ACT.Abs_reciprocal_sqrt, scale=1.0 / (D_MODEL - 1), bias=TINY
+            )
+            nc.scalar.activation(out=sigma_n[:], in_=ssq[:], func=ACT.Copy, scale=inv_sigma[:])
+            nc.scalar.activation(
+                out=shifted_sq[:], in_=sigma_n[:], func=ACT.Square, scale=1.0 / (D_MODEL - 1), bias=EPS
+            )
+            nc.scalar.activation(out=rstd[:], in_=shifted_sq[:], func=ACT.Abs_reciprocal_sqrt)
             small[i]["rstd"] = rstd
 
         def vector_pieces(whole_row):
@@ -292,7 +295,6 @@ def tile_multiheadattention_pa_kernel(
             if i + 3 < N_TILES:
                 transpose_only(i + 3)
             if before:
-                inverse_deviation(i - 1)
                 vector_bias(i - 1, i - 1 == last)
             if before and i - 1 != last:
                 gpsimd_rest(i - 1)

@@ -29,7 +29,8 @@ BANK = 512
 BANKS_PER_ROW = D_MODEL // BANK
 EPS = 1e-3
 TINY = 1e-30
-VECTOR_COLS = 704
+VECTOR_COLS = 512
+SHARED_TILES = 6
 
 FLOPS = 2 * TOKENS * (HEADS * HALF) * D_MODEL
 
@@ -41,12 +42,12 @@ def tile_multiheadattention_pa_kernel(
     with ExitStack() as stack:
         const = stack.enter_context(tc.tile_pool(name="const", bufs=1))
         loads = stack.enter_context(tc.tile_pool(name="loads", bufs=N_TILES))
-        stage = stack.enter_context(tc.tile_pool(name="stage", bufs=3))
-        rows = stack.enter_context(tc.tile_pool(name="rows", bufs=3))
+        stage = stack.enter_context(tc.tile_pool(name="stage", bufs=4))
+        rows = stack.enter_context(tc.tile_pool(name="rows", bufs=4))
         results = stack.enter_context(tc.tile_pool(name="results", bufs=N_TILES))
         stats = stack.enter_context(tc.tile_pool(name="stats", bufs=4))
         xt_psum = stack.enter_context(tc.psum_pool(name="xt_psum", bufs=2))
-        z_psum = stack.enter_context(tc.psum_pool(name="z_psum", bufs=1))
+        z_psum = stack.enter_context(tc.psum_pool(name="z_psum", bufs=2))
         ab_psum = stack.enter_context(tc.psum_pool(name="ab_psum", bufs=1))
         stack.enter_context(tc.manual_schedule())
 
@@ -142,10 +143,6 @@ def tile_multiheadattention_pa_kernel(
             nc.scalar.copy(out=grouped_words, in_=xt[:].rearrange("p g u r -> p g r u"))
             grouped_tiles[i] = grouped
 
-        def transpose_tile(i):
-            transpose_only(i)
-            copy_out(i)
-
         def quantise_tile(i):
             codes = stage.tile([P, PASSES * P], U32, align_bytes=64)
             code_scales = stage.tile([P, PASSES * P], U8, align_bytes=64)
@@ -205,104 +202,150 @@ def tile_multiheadattention_pa_kernel(
             )
             small[i]["ssq"] = ssq
 
-        def deviation(i):
-            ssq = small[i]["ssq"]
-            inv_sigma = stats.tile([P, 1], F32)
-            sigma_n = stats.tile([P, 1], F32)
-            shifted_sq = stats.tile([P, 1], F32)
-            rstd = stats.tile([P, 1], F32)
-            nc.scalar.activation(
-                out=inv_sigma[:], in_=ssq[:], func=ACT.Abs_reciprocal_sqrt, scale=1.0 / (D_MODEL - 1), bias=TINY
-            )
-            nc.scalar.activation(out=sigma_n[:], in_=ssq[:], func=ACT.Copy, scale=inv_sigma[:])
-            nc.scalar.activation(
-                out=shifted_sq[:], in_=sigma_n[:], func=ACT.Square, scale=1.0 / (D_MODEL - 1), bias=EPS
-            )
-            nc.scalar.activation(out=rstd[:], in_=shifted_sq[:], func=ACT.Abs_reciprocal_sqrt)
-            small[i]["rstd"] = rstd
+        def deviation_step(i, step):
+            if step == 0:
+                inv_sigma = stats.tile([P, 1], F32)
+                nc.scalar.activation(
+                    out=inv_sigma[:],
+                    in_=small[i]["ssq"][:],
+                    func=ACT.Abs_reciprocal_sqrt,
+                    scale=1.0 / (D_MODEL - 1),
+                    bias=TINY,
+                )
+                small[i]["inv_sigma"] = inv_sigma
+            if step == 1:
+                sigma_n = stats.tile([P, 1], F32)
+                nc.scalar.activation(
+                    out=sigma_n[:], in_=small[i]["ssq"][:], func=ACT.Copy, scale=small[i]["inv_sigma"][:]
+                )
+                small[i]["sigma_n"] = sigma_n
+            if step == 2:
+                shifted_sq = stats.tile([P, 1], F32)
+                nc.scalar.activation(
+                    out=shifted_sq[:], in_=small[i]["sigma_n"][:], func=ACT.Square, scale=1.0 / (D_MODEL - 1), bias=EPS
+                )
+                small[i]["shifted_sq"] = shifted_sq
+            if step == 3:
+                rstd = stats.tile([P, 1], F32)
+                nc.scalar.activation(out=rstd[:], in_=small[i]["shifted_sq"][:], func=ACT.Abs_reciprocal_sqrt)
+                small[i]["rstd"] = rstd
 
-        def vector_pieces(whole_row):
-            end = D_MODEL if whole_row else VECTOR_COLS
-            return [(0, 0, BANK), (1, BANK, end - BANK)]
+        def shared(i):
+            return i < SHARED_TILES
 
-        def vector_gain(i, whole_row):
-            o_row = results.tile([P, D_MODEL], F32)
-            o_rows[i] = o_row
-            for c, first, width in vector_pieces(whole_row):
+        def vector_pieces(i):
+            pieces = [(0, gain_bias[:, 0, :], gain_bias[:, 1, :])]
+            if not shared(i):
+                pieces.append((BANK, high_banks[0][:], high_banks[1][:]))
+            return pieces
+
+        def vector_gain(i):
+            for first, gain, unused in vector_pieces(i):
                 nc.vector.scalar_tensor_tensor(
-                    out=o_row[:, first : first + width],
-                    in0=z_rows[i][:, first : first + width],
+                    out=o_rows[i][:, first : first + BANK],
+                    in0=z_rows[i][:, first : first + BANK],
                     scalar=small[i]["neg_mean"][:],
-                    in1=gain_bias[:, 0, c, 0:width],
+                    in1=gain,
                     op0=ALU.add,
                     op1=ALU.mult,
                 )
 
-        def vector_bias(i, whole_row):
-            for c, first, width in vector_pieces(whole_row):
+        def vector_bias(i):
+            for first, unused, bias in vector_pieces(i):
                 nc.vector.scalar_tensor_tensor(
-                    out=o_rows[i][:, first : first + width],
-                    in0=o_rows[i][:, first : first + width],
+                    out=o_rows[i][:, first : first + BANK],
+                    in0=o_rows[i][:, first : first + BANK],
                     scalar=small[i]["rstd"][:],
-                    in1=gain_bias[:, 1, c, 0:width],
+                    in1=bias,
                     op0=ALU.mult,
                     op1=ALU.add,
                 )
+                store_piece(i, first)
 
-        def gpsimd_rest(i):
-            rest = o_rows[i][:, VECTOR_COLS:]
-            nc.gpsimd.tensor_scalar(
-                out=rest,
-                in0=z_rows[i][:, VECTOR_COLS:],
-                scalar1=small[i]["neg_mean"][:],
-                scalar2=small[i]["rstd"][:],
-                op0=ALU.add,
-                op1=ALU.mult,
+        def normalise_shift(i):
+            shift = stats.tile([P, 1], F32)
+            nc.scalar.activation(out=shift[:], in_=small[i]["neg_mean"][:], func=ACT.Copy, scale=small[i]["rstd"][:])
+            small[i]["shift"] = shift
+
+        def scalar_normalise(i):
+            nc.scalar.activation(
+                out=o_rows[i][:, VECTOR_COLS:],
+                in_=z_rows[i][:, VECTOR_COLS:],
+                func=ACT.Identity,
+                scale=small[i]["rstd"][:],
+                bias=small[i]["shift"][:],
             )
+
+        def gpsimd_gain_bias(i):
+            rest = o_rows[i][:, VECTOR_COLS:]
             nc.gpsimd.tensor_tensor(out=rest, in0=rest, in1=ab_high[:, 0, :], op=ALU.mult)
             nc.gpsimd.tensor_tensor(out=rest, in0=rest, in1=ab_high[:, 1, :], op=ALU.add)
 
-        def store_tile(i):
-            nc.sync.dma_start(out=out[P * i : P * (i + 1), :], in_=o_rows[i][:])
+        def store_piece(i, first):
+            nc.sync.dma_start(out=out[P * i : P * (i + 1), first : first + BANK], in_=o_rows[i][:, first : first + BANK])
 
-        transpose_tile(0)
+        def spread(bank, v, c):
+            first = D_MODEL * v + BANK * c
+            nc.tensor.matmul(bank, lhsT=ones[:], rhs=ab_rows[:, first : first + BANK], start=True, stop=True)
+
+        transpose_only(0)
+        copy_out(0)
         quantise_tile(0)
-        gain_bias = ab_psum.tile([P, 2, BANKS_PER_ROW, BANK], F32)
+        gain_bias = ab_psum.tile([P, 2, BANK], F32)
         ab_high = const.tile([P, 2, D_MODEL - VECTOR_COLS], F32)
+        lent = z_psum.tile([P, 2, BANK], F32, tag="z")
         for v in range(2):
-            for c in range(BANKS_PER_ROW):
-                first = D_MODEL * v + BANK * c
-                nc.tensor.matmul(
-                    gain_bias[:, v, c, :], lhsT=ones[:], rhs=ab_rows[:, first : first + BANK], start=True, stop=True
-                )
-            nc.scalar.copy(out=ab_high[:, v, :], in_=gain_bias[:, v, 1, VECTOR_COLS - BANK :])
+            spread(gain_bias[:, v, :], v, 0)
+            spread(lent[:, v, :], v, 1)
+            nc.scalar.copy(out=ab_high[:, v, :], in_=lent[:, v, :])
         project_tile(0)
-        transpose_tile(1)
-        transpose_tile(2)
+        for i in (1, 2):
+            transpose_only(i)
+            copy_out(i)
 
-        last = N_TILES - 1
-        for i in range(N_TILES + 1):
-            now = i < N_TILES
-            before = i >= 1
-            if i + 1 < N_TILES:
-                quantise_tile(i + 1)
-            if now:
-                add_residual(i, 0)
-                add_residual(i, 1)
-                negative_mean(i)
-            if i + 1 < N_TILES:
-                project_tile(i + 1)
-            if i + 3 < N_TILES:
-                transpose_only(i + 3)
-            if before:
-                vector_bias(i - 1, i - 1 == last)
-            if before and i - 1 != last:
-                gpsimd_rest(i - 1)
-            if before:
-                store_tile(i - 1)
-            if now:
-                vector_gain(i, i == last)
-                sum_of_squares(i)
-                deviation(i)
-            if i + 3 < N_TILES:
-                copy_out(i + 3)
+        def tile_is(i):
+            return 0 <= i < N_TILES
+
+        high_banks = []
+        for r in range(N_TILES + 2):
+            if tile_is(r + 3):
+                transpose_only(r + 3)
+            if r + 3 == N_TILES:
+                for v in range(2):
+                    high = xt_psum.tile([P, BANK], F32, tag="xt")
+                    spread(high[:], v, 1)
+                    high_banks.append(high)
+            if tile_is(r):
+                o_row = results.tile([P, D_MODEL], F32)
+                o_rows[r] = o_row
+                add_residual(r, 0)
+            if tile_is(r + 1):
+                quantise_tile(r + 1)
+                project_tile(r + 1)
+            if tile_is(r - 1):
+                vector_gain(r - 1)
+            if tile_is(r):
+                add_residual(r, 1)
+            if tile_is(r - 2):
+                vector_bias(r - 2)
+            if tile_is(r - 4) and shared(r - 4):
+                store_piece(r - 4, VECTOR_COLS)
+            if tile_is(r):
+                negative_mean(r)
+            if tile_is(r - 2) and shared(r - 2):
+                normalise_shift(r - 2)
+            if tile_is(r - 1):
+                deviation_step(r - 1, 0)
+            if tile_is(r + 3):
+                copy_out(r + 3)
+            if tile_is(r - 1):
+                deviation_step(r - 1, 1)
+            if tile_is(r):
+                sum_of_squares(r)
+            if tile_is(r - 1):
+                deviation_step(r - 1, 2)
+            if tile_is(r - 2) and shared(r - 2):
+                scalar_normalise(r - 2)
+                gpsimd_gain_bias(r - 2)
+            if tile_is(r - 1):
+                deviation_step(r - 1, 3)

@@ -47,7 +47,7 @@ def tile_multiheadattention_pa_kernel(
         results = stack.enter_context(tc.tile_pool(name="results", bufs=N_TILES))
         stats = stack.enter_context(tc.tile_pool(name="stats", bufs=4))
         xt_psum = stack.enter_context(tc.psum_pool(name="xt_psum", bufs=2))
-        z_psum = stack.enter_context(tc.psum_pool(name="z_psum", bufs=2))
+        z_psum = stack.enter_context(tc.psum_pool(name="z_psum", bufs=1))
         ab_psum = stack.enter_context(tc.psum_pool(name="ab_psum", bufs=1))
         stack.enter_context(tc.manual_schedule())
 
@@ -153,21 +153,20 @@ def tile_multiheadattention_pa_kernel(
             )
             code_tiles[i] = (codes, code_scales)
 
-        def project_tile(i):
+        def project_half(i, c):
             codes, code_scales = code_tiles[i]
-            z = z_psum.tile([P, BANKS_PER_ROW, BANK], F32)
-            for c in range(BANKS_PER_ROW):
-                for g in range(PASSES):
-                    nc.tensor.matmul_mx(
-                        out=z[:, c, :],
-                        lhsT=codes[:, P * g : P * (g + 1)].bitcast(FP8X4),
-                        lhsT_scale=code_scales[:, P * g : P * (g + 1)],
-                        rhs=w_both[:, g, 2 * BANK * c : 2 * BANK * (c + 1)].bitcast(FP4X4),
-                        rhs_scale=w_scales[:, g, BANK * c : BANK * (c + 1)],
-                        start=(g == 0),
-                        stop=(g == PASSES - 1),
-                    )
-            z_banks[i] = z
+            z = z_psum.tile([P, BANK], F32, tag="z%d" % c)
+            for g in range(PASSES):
+                nc.tensor.matmul_mx(
+                    out=z[:],
+                    lhsT=codes[:, P * g : P * (g + 1)].bitcast(FP8X4),
+                    lhsT_scale=code_scales[:, P * g : P * (g + 1)],
+                    rhs=w_both[:, g, 2 * BANK * c : 2 * BANK * (c + 1)].bitcast(FP4X4),
+                    rhs_scale=w_scales[:, g, BANK * c : BANK * (c + 1)],
+                    start=(g == 0),
+                    stop=(g == PASSES - 1),
+                )
+            z_banks[(i, c)] = z
 
         def add_residual(i, c):
             if c == 0:
@@ -178,7 +177,7 @@ def tile_multiheadattention_pa_kernel(
             cols = slice(BANK * c, BANK * (c + 1))
             nc.vector.scalar_tensor_tensor(
                 out=z_rows[i][:, cols],
-                in0=z_banks[i][:, c, :],
+                in0=z_banks[(i, c)][:],
                 scalar=1.0,
                 in1=inp_tiles[i][:, cols],
                 op0=ALU.mult,
@@ -204,28 +203,22 @@ def tile_multiheadattention_pa_kernel(
 
         def deviation_step(i, step):
             if step == 0:
-                inv_sigma = stats.tile([P, 1], F32)
+                inv_root = stats.tile([P, 1], F32)
                 nc.scalar.activation(
-                    out=inv_sigma[:],
+                    out=inv_root[:],
                     in_=small[i]["ssq"][:],
                     func=ACT.Abs_reciprocal_sqrt,
-                    scale=1.0 / (D_MODEL - 1),
+                    scale=float(D_MODEL - 1),
                     bias=TINY,
                 )
-                small[i]["inv_sigma"] = inv_sigma
+                small[i]["inv_root"] = inv_root
             if step == 1:
-                sigma_n = stats.tile([P, 1], F32)
-                nc.scalar.activation(
-                    out=sigma_n[:], in_=small[i]["ssq"][:], func=ACT.Copy, scale=small[i]["inv_sigma"][:]
-                )
-                small[i]["sigma_n"] = sigma_n
-            if step == 2:
                 shifted_sq = stats.tile([P, 1], F32)
                 nc.scalar.activation(
-                    out=shifted_sq[:], in_=small[i]["sigma_n"][:], func=ACT.Square, scale=1.0 / (D_MODEL - 1), bias=EPS
+                    out=shifted_sq[:], in_=small[i]["ssq"][:], func=ACT.Square, scale=small[i]["inv_root"][:], bias=EPS
                 )
                 small[i]["shifted_sq"] = shifted_sq
-            if step == 3:
+            if step == 2:
                 rstd = stats.tile([P, 1], F32)
                 nc.scalar.activation(out=rstd[:], in_=small[i]["shifted_sq"][:], func=ACT.Abs_reciprocal_sqrt)
                 small[i]["rstd"] = rstd
@@ -234,9 +227,9 @@ def tile_multiheadattention_pa_kernel(
             return i < SHARED_TILES
 
         def vector_pieces(i):
-            pieces = [(0, gain_bias[:, 0, :], gain_bias[:, 1, :])]
+            pieces = [(0, gain_bias[:, 0, 0, :], gain_bias[:, 1, 0, :])]
             if not shared(i):
-                pieces.append((BANK, high_banks[0][:], high_banks[1][:]))
+                pieces.append((BANK, gain_bias[:, 0, 1, :], gain_bias[:, 1, 1, :]))
             return pieces
 
         def vector_gain(i):
@@ -291,14 +284,14 @@ def tile_multiheadattention_pa_kernel(
         transpose_only(0)
         copy_out(0)
         quantise_tile(0)
-        gain_bias = ab_psum.tile([P, 2, BANK], F32)
+        gain_bias = ab_psum.tile([P, 2, BANKS_PER_ROW, BANK], F32)
         ab_high = const.tile([P, 2, D_MODEL - VECTOR_COLS], F32)
-        lent = z_psum.tile([P, 2, BANK], F32, tag="z")
         for v in range(2):
-            spread(gain_bias[:, v, :], v, 0)
-            spread(lent[:, v, :], v, 1)
-            nc.scalar.copy(out=ab_high[:, v, :], in_=lent[:, v, :])
-        project_tile(0)
+            for c in range(BANKS_PER_ROW):
+                spread(gain_bias[:, v, c, :], v, c)
+            nc.scalar.copy(out=ab_high[:, v, :], in_=gain_bias[:, v, 1, :])
+        project_half(0, 0)
+        project_half(0, 1)
         for i in (1, 2):
             transpose_only(i)
             copy_out(i)
@@ -306,26 +299,24 @@ def tile_multiheadattention_pa_kernel(
         def tile_is(i):
             return 0 <= i < N_TILES
 
-        high_banks = []
         for r in range(N_TILES + 2):
-            if tile_is(r + 3):
-                transpose_only(r + 3)
-            if r + 3 == N_TILES:
-                for v in range(2):
-                    high = xt_psum.tile([P, BANK], F32, tag="xt")
-                    spread(high[:], v, 1)
-                    high_banks.append(high)
             if tile_is(r):
                 o_row = results.tile([P, D_MODEL], F32)
                 o_rows[r] = o_row
                 add_residual(r, 0)
             if tile_is(r + 1):
                 quantise_tile(r + 1)
-                project_tile(r + 1)
+                project_half(r + 1, 0)
+            if r > 0 and tile_is(r + 3):
+                transpose_only(r + 3)
             if tile_is(r - 1):
                 vector_gain(r - 1)
             if tile_is(r):
                 add_residual(r, 1)
+            if tile_is(r + 1):
+                project_half(r + 1, 1)
+            if r == 0:
+                transpose_only(r + 3)
             if tile_is(r - 2):
                 vector_bias(r - 2)
             if tile_is(r - 4) and shared(r - 4):
@@ -338,14 +329,15 @@ def tile_multiheadattention_pa_kernel(
                 deviation_step(r - 1, 0)
             if tile_is(r + 3):
                 copy_out(r + 3)
+            if r == N_TILES - 1 and shared(r - 2):
+                scalar_normalise(r - 2)
+                gpsimd_gain_bias(r - 2)
             if tile_is(r - 1):
                 deviation_step(r - 1, 1)
             if tile_is(r):
                 sum_of_squares(r)
             if tile_is(r - 1):
                 deviation_step(r - 1, 2)
-            if tile_is(r - 2) and shared(r - 2):
+            if r != N_TILES - 1 and tile_is(r - 2) and shared(r - 2):
                 scalar_normalise(r - 2)
                 gpsimd_gain_bias(r - 2)
-            if tile_is(r - 1):
-                deviation_step(r - 1, 3)

@@ -329,15 +329,12 @@ def tile_multiheadattention_pa_kernel(
                 deviation_step(r - 1, 0)
             if tile_is(r + 3):
                 copy_out(r + 3)
-            if r == N_TILES - 1 and shared(r - 2):
-                scalar_normalise(r - 2)
-                gpsimd_gain_bias(r - 2)
             if tile_is(r - 1):
                 deviation_step(r - 1, 1)
-            if tile_is(r):
-                sum_of_squares(r)
-            if tile_is(r - 1):
-                deviation_step(r - 1, 2)
-            if r != N_TILES - 1 and tile_is(r - 2) and shared(r - 2):
+            if tile_is(r - 2) and shared(r - 2):
                 scalar_normalise(r - 2)
                 gpsimd_gain_bias(r - 2)
+            if tile_is(r - 1):
+                deviation_step(r - 1, 2)
+            if tile_is(r):
+                sum_of_squares(r)

@@ -285,7 +285,7 @@ def tile_multiheadattention_pa_kernel(
         copy_out(0)
         quantise_tile(0)
         gain_bias = ab_psum.tile([P, 2, BANKS_PER_ROW, BANK], F32)
-        ab_high = const.tile([P, 2, D_MODEL - VECTOR_COLS], F32)
+        ab_high = const.tile([P, 2, D_MODEL - VECTOR_COLS], BF16)
         for v in range(2):
             for c in range(BANKS_PER_ROW):
                 spread(gain_bias[:, v, c, :], v, c)

@@ -31,6 +31,7 @@ EPS = 1e-3
 TINY = 1e-30
 VECTOR_COLS = 512
 SHARED_TILES = 6
+LAST_SHARED_COLS = 768
 
 FLOPS = 2 * TOKENS * (HEADS * HALF) * D_MODEL
 
@@ -226,34 +227,37 @@ def tile_multiheadattention_pa_kernel(
         def shared(i):
             return i < SHARED_TILES
 
+        def vector_cols(i):
+            if i == SHARED_TILES - 1:
+                return LAST_SHARED_COLS
+            return VECTOR_COLS if shared(i) else D_MODEL
+
         def vector_pieces(i):
-            pieces = [(0, gain_bias[:, 0, 0, :], gain_bias[:, 1, 0, :])]
-            if not shared(i):
-                pieces.append((BANK, gain_bias[:, 0, 1, :], gain_bias[:, 1, 1, :]))
-            return pieces
+            widths = [min(BANK, vector_cols(i) - BANK * c) for c in range(BANKS_PER_ROW)]
+            return [(BANK * c, widths[c], c) for c in range(BANKS_PER_ROW) if widths[c] > 0]
 
         def vector_gain(i):
-            for first, gain, unused in vector_pieces(i):
+            for first, width, c in vector_pieces(i):
                 nc.vector.scalar_tensor_tensor(
-                    out=o_rows[i][:, first : first + BANK],
-                    in0=z_rows[i][:, first : first + BANK],
+                    out=o_rows[i][:, first : first + width],
+                    in0=z_rows[i][:, first : first + width],
                     scalar=small[i]["neg_mean"][:],
-                    in1=gain,
+                    in1=gain_bias[:, 0, c, 0:width],
                     op0=ALU.add,
                     op1=ALU.mult,
                 )
 
         def vector_bias(i):
-            for first, unused, bias in vector_pieces(i):
+            for first, width, c in vector_pieces(i):
                 nc.vector.scalar_tensor_tensor(
-                    out=o_rows[i][:, first : first + BANK],
-                    in0=o_rows[i][:, first : first + BANK],
+                    out=o_rows[i][:, first : first + width],
+                    in0=o_rows[i][:, first : first + width],
                     scalar=small[i]["rstd"][:],
-                    in1=bias,
+                    in1=gain_bias[:, 1, c, 0:width],
                     op0=ALU.mult,
                     op1=ALU.add,
                 )
-                store_piece(i, first)
+                store_piece(i, first, width)
 
         def normalise_shift(i):
             shift = stats.tile([P, 1], F32)
@@ -262,20 +266,22 @@ def tile_multiheadattention_pa_kernel(
 
         def scalar_normalise(i):
             nc.scalar.activation(
-                out=o_rows[i][:, VECTOR_COLS:],
-                in_=z_rows[i][:, VECTOR_COLS:],
+                out=o_rows[i][:, vector_cols(i) :],
+                in_=z_rows[i][:, vector_cols(i) :],
                 func=ACT.Identity,
                 scale=small[i]["rstd"][:],
                 bias=small[i]["shift"][:],
             )
 
         def gpsimd_gain_bias(i):
-            rest = o_rows[i][:, VECTOR_COLS:]
-            nc.gpsimd.tensor_tensor(out=rest, in0=rest, in1=ab_high[:, 0, :], op=ALU.mult)
-            nc.gpsimd.tensor_tensor(out=rest, in0=rest, in1=ab_high[:, 1, :], op=ALU.add)
+            rest = o_rows[i][:, vector_cols(i) :]
+            nc.gpsimd.tensor_tensor(out=rest, in0=rest, in1=ab_high[:, 0, vector_cols(i) - VECTOR_COLS :], op=ALU.mult)
+            nc.gpsimd.tensor_tensor(out=rest, in0=rest, in1=ab_high[:, 1, vector_cols(i) - VECTOR_COLS :], op=ALU.add)
 
-        def store_piece(i, first):
-            nc.sync.dma_start(out=out[P * i : P * (i + 1), first : first + BANK], in_=o_rows[i][:, first : first + BANK])
+        def store_piece(i, first, width):
+            nc.sync.dma_start(
+                out=out[P * i : P * (i + 1), first : first + width], in_=o_rows[i][:, first : first + width]
+            )
 
         def spread(bank, v, c):
             first = D_MODEL * v + BANK * c
@@ -320,7 +326,7 @@ def tile_multiheadattention_pa_kernel(
             if tile_is(r - 2):
                 vector_bias(r - 2)
             if tile_is(r - 4) and shared(r - 4):
-                store_piece(r - 4, VECTOR_COLS)
+                store_piece(r - 4, vector_cols(r - 4), D_MODEL - vector_cols(r - 4))
             if tile_is(r):
                 negative_mean(r)
             if tile_is(r - 2) and shared(r - 2):
@@ -331,10 +337,13 @@ def tile_multiheadattention_pa_kernel(
                 copy_out(r + 3)
             if tile_is(r - 1):
                 deviation_step(r - 1, 1)
+            last_round = r == N_TILES - 1
+            if last_round:
+                sum_of_squares(r)
             if tile_is(r - 2) and shared(r - 2):
                 scalar_normalise(r - 2)
                 gpsimd_gain_bias(r - 2)
             if tile_is(r - 1):
                 deviation_step(r - 1, 2)
-            if tile_is(r):
+            if tile_is(r) and not last_round:
                 sum_of_squares(r)

@@ -54,19 +54,25 @@ def tile_multiheadattention_pa_kernel(
 
         w_both = const.tile([P, PASSES, 2 * D_MODEL], U8, align_bytes=64)
         w_scales = const.tile([P, PASSES, D_MODEL], U8, align_bytes=64)
-        ab_rows = const.tile([P, 2 * D_MODEL], BF16)
-        ones = const.tile([P, P], BF16)
+        ab_rows = const.tile([P, BANK], BF16)
         one = const.tile([P, 1], F32)
-        nc.vector.memset(w_both[:].bitcast(I32), 0)
-        nc.vector.memset(w_scales[:].bitcast(I32), 0)
-        nc.vector.memset(ones[:], 1.0)
+        words_sb = w_both[:].bitcast(I32)
+        scales_sb = w_scales[:].bitcast(I32)
+        split_w = D_CONTENT // 2
+        split_s = D_CONTENT // 4
+        nc.vector.memset(ab_rows[:].bitcast(F32), 0.0)
         nc.vector.memset(one[:], 1.0)
-
-        nc.gpsimd.memset(ab_rows[:].bitcast(F32), 0.0)
-        nc.scalar.dma_start(out=ab_rows[0:1, 0:D_MODEL], in_=ln_a.rearrange("(o n) -> o n", o=1))
-        nc.scalar.dma_start(out=ab_rows[0:1, D_MODEL : 2 * D_MODEL], in_=ln_b.rearrange("(o n) -> o n", o=1))
+        nc.vector.memset(words_sb[:, :, 0:split_w], 0)
+        nc.vector.memset(scales_sb, 0)
         ident = const.tile([P, P], F32)
         make_identity(nc, ident[:])
+        nc.gpsimd.memset(words_sb[:, :, split_w:], 0)
+
+        for v, vec in enumerate((ln_a, ln_b)):
+            nc.scalar.dma_start(
+                out=ab_rows[BANKS_PER_ROW * v : BANKS_PER_ROW * (v + 1), :],
+                in_=vec.rearrange("(c n) -> c n", c=BANKS_PER_ROW),
+            )
 
         warm = const.tile([P, 1], F32)
         nc.scalar.activation(out=warm[:], in_=one[:], func=ACT.Abs_reciprocal_sqrt)
@@ -75,46 +81,46 @@ def tile_multiheadattention_pa_kernel(
         x_tiles = []
         inp_tiles = []
 
-        def load_x(i):
+        def load_x(i, queue):
             x_tile = loads.tile([P, HEADS, D_V], BF16)
-            nc.sync.dma_start(out=x_tile[:], in_=x_src[:, P * i : P * (i + 1), :].rearrange("h p f -> p h f"))
+            queue.dma_start(out=x_tile[:], in_=x_src[:, P * i : P * (i + 1), :].rearrange("h p f -> p h f"))
             x_tiles.append(x_tile)
 
-        def load_inp(i):
+        def load_inp(i, queue):
             inp_tile = loads.tile([P, D_MODEL], BF16)
-            nc.sync.dma_start(out=inp_tile[:], in_=inp[P * i : P * (i + 1), :])
+            queue.dma_start(out=inp_tile[:], in_=inp[P * i : P * (i + 1), :])
             inp_tiles.append(inp_tile)
 
         def load_weights():
-            words_sb = w_both[:].bitcast(I32)
-            scales_sb = w_scales[:].bitcast(I32)
-            split_w = D_CONTENT // 2
-            split_s = D_CONTENT // 4
             w1 = w_proj1_words[0].bitcast(I32).rearrange("(g h q) w -> h q g w", g=PASSES, h=HEADS_PER_PASS)
             w2 = w_proj2_words[0].bitcast(I32).rearrange("(g h q) w -> h q g w", g=PASSES, h=HEADS_PER_PASS)
+            s1 = w_proj1_scales[0].bitcast(I32).rearrange("(g h e) w -> e h g w", g=PASSES, h=HEADS_PER_PASS)
+            s2 = w_proj2_scales[0].bitcast(I32).rearrange("(g h e) w -> e h g w", g=PASSES, h=HEADS_PER_PASS)
             for h in range(HEADS_PER_PASS):
                 first = 2 * ROWS_PER_HALF * h
                 nc.sync.dma_start(out=words_sb[first : first + ROWS_PER_HALF, :, 0:split_w], in_=w1[h])
-                nc.sync.dma_start(
-                    out=words_sb[first + ROWS_PER_HALF : first + 2 * ROWS_PER_HALF, :, split_w:], in_=w2[h]
-                )
-            s1 = w_proj1_scales[0].bitcast(I32).rearrange("(g h e) w -> e h g w", g=PASSES, h=HEADS_PER_PASS)
-            s2 = w_proj2_scales[0].bitcast(I32).rearrange("(g h e) w -> e h g w", g=PASSES, h=HEADS_PER_PASS)
             for e in range(2):
                 nc.sync.dma_start(out=scales_sb[e : P : 32, :, 0:split_s], in_=s1[e])
+            load_x(1, nc.sync)
+            for h in range(HEADS_PER_PASS):
+                first = 2 * ROWS_PER_HALF * h + ROWS_PER_HALF
+                nc.sync.dma_start(out=words_sb[first : first + ROWS_PER_HALF, :, split_w:], in_=w2[h])
+            for e in range(2):
                 nc.sync.dma_start(out=scales_sb[2 + e : P : 32, :, split_s:], in_=s2[e])
 
-        load_x(0)
+        load_x(0, nc.sync)
+        load_inp(0, nc.gpsimd)
         load_weights()
-        for i in range(N_TILES):
+        for i in range(1, N_TILES):
             if i + 1 < N_TILES:
-                load_x(i + 1)
-            load_inp(i)
+                load_x(i + 1, nc.sync)
+            load_inp(i, nc.sync)
 
         xt_banks = {}
         grouped_tiles = {}
         code_tiles = {}
         z_banks = {}
+        ab_banks = {}
         z_rows = {}
         o_rows = {}
         small = {}
@@ -242,7 +248,7 @@ def tile_multiheadattention_pa_kernel(
                     out=o_rows[i][:, first : first + width],
                     in0=z_rows[i][:, first : first + width],
                     scalar=small[i]["neg_mean"][:],
-                    in1=gain_bias[:, 0, c, 0:width],
+                    in1=ab_banks[(0, c)][:, 0:width],
                     op0=ALU.add,
                     op1=ALU.mult,
                 )
@@ -253,7 +259,7 @@ def tile_multiheadattention_pa_kernel(
                     out=o_rows[i][:, first : first + width],
                     in0=o_rows[i][:, first : first + width],
                     scalar=small[i]["rstd"][:],
-                    in1=gain_bias[:, 1, c, 0:width],
+                    in1=ab_banks[(1, c)][:, 0:width],
                     op0=ALU.mult,
                     op1=ALU.add,
                 )
@@ -283,24 +289,33 @@ def tile_multiheadattention_pa_kernel(
                 out=out[P * i : P * (i + 1), first : first + width], in_=o_rows[i][:, first : first + width]
             )
 
-        def spread(bank, v, c):
-            first = D_MODEL * v + BANK * c
-            nc.tensor.matmul(bank, lhsT=ones[:], rhs=ab_rows[:, first : first + BANK], start=True, stop=True)
+        ident_bf = ident[:].bitcast(BF16)
+
+        def spread(v, c):
+            row = BANKS_PER_ROW * v + c
+            bank = ab_psum.tile([P, BANK], F32, tag="ab%d%d" % (v, c))
+            nc.tensor.matmul(
+                bank[:],
+                lhsT=ident_bf[:, 2 * row + 1 : 2 * row + 2].to_broadcast([P, P]),
+                rhs=ab_rows[:],
+                start=True,
+                stop=True,
+            )
+            ab_banks[(v, c)] = bank
 
         transpose_only(0)
         copy_out(0)
         quantise_tile(0)
-        gain_bias = ab_psum.tile([P, 2, BANKS_PER_ROW, BANK], F32)
         ab_high = const.tile([P, 2, D_MODEL - VECTOR_COLS], BF16)
         for v in range(2):
-            for c in range(BANKS_PER_ROW):
-                spread(gain_bias[:, v, c, :], v, c)
-            nc.scalar.copy(out=ab_high[:, v, :], in_=gain_bias[:, v, 1, :])
+            spread(v, 1)
+            nc.scalar.copy(out=ab_high[:, v, :], in_=ab_banks[(v, 1)][:])
         project_half(0, 0)
+        transpose_only(1)
+        copy_out(1)
         project_half(0, 1)
-        for i in (1, 2):
-            transpose_only(i)
-            copy_out(i)
+        for v in range(2):
+            spread(v, 0)
 
         def tile_is(i):
             return 0 <= i < N_TILES
@@ -310,40 +325,45 @@ def tile_multiheadattention_pa_kernel(
                 o_row = results.tile([P, D_MODEL], F32)
                 o_rows[r] = o_row
                 add_residual(r, 0)
+            if r == 0:
+                add_residual(r, 1)
             if tile_is(r + 1):
                 quantise_tile(r + 1)
                 project_half(r + 1, 0)
-            if r > 0 and tile_is(r + 3):
+            if r == 0:
+                transpose_only(2)
+            elif tile_is(r + 3):
                 transpose_only(r + 3)
             if tile_is(r - 1):
                 vector_gain(r - 1)
-            if tile_is(r):
+            if tile_is(r) and r > 0:
                 add_residual(r, 1)
             if tile_is(r + 1):
                 project_half(r + 1, 1)
             if r == 0:
-                transpose_only(r + 3)
+                transpose_only(3)
             if tile_is(r - 2):
                 vector_bias(r - 2)
-            if tile_is(r - 4) and shared(r - 4):
-                store_piece(r - 4, vector_cols(r - 4), D_MODEL - vector_cols(r - 4))
+            if tile_is(r - 3) and shared(r - 3):
+                store_piece(r - 3, vector_cols(r - 3), D_MODEL - vector_cols(r - 3))
             if tile_is(r):
                 negative_mean(r)
-            if tile_is(r - 2) and shared(r - 2):
-                normalise_shift(r - 2)
-            if tile_is(r - 1):
-                deviation_step(r - 1, 0)
-            if tile_is(r + 3):
-                copy_out(r + 3)
-            if tile_is(r - 1):
-                deviation_step(r - 1, 1)
-            last_round = r == N_TILES - 1
-            if last_round:
-                sum_of_squares(r)
-            if tile_is(r - 2) and shared(r - 2):
-                scalar_normalise(r - 2)
-                gpsimd_gain_bias(r - 2)
             if tile_is(r - 1):
                 deviation_step(r - 1, 2)
-            if tile_is(r) and not last_round:
+            if tile_is(r):
                 sum_of_squares(r)
+            if tile_is(r - 1) and shared(r - 1):
+                normalise_shift(r - 1)
+            if r == 0:
+                copy_out(2)
+            elif tile_is(r + 3):
+                copy_out(r + 3)
+            if tile_is(r):
+                deviation_step(r, 0)
+            if r == 0:
+                copy_out(3)
+            if tile_is(r - 1) and shared(r - 1):
+                scalar_normalise(r - 1)
+                gpsimd_gain_bias(r - 1)
+            if tile_is(r):
+                deviation_step(r, 1)

@@ -27,10 +27,19 @@ HEADS_PER_PASS = HEADS // PASSES
 ROWS_PER_HALF = HALF // PACK
 BANK = 512
 BANKS_PER_ROW = D_MODEL // BANK
+WIDTHS = (D_CONTENT, D_MODEL - D_CONTENT)
+GROUP = 128
+COLUMN_GROUPS = (
+    ((0, 0, BANK, 0),),
+    tuple((0, BANK + n, GROUP, n) for n in range(0, D_CONTENT - BANK, GROUP))
+    + tuple((1, n, GROUP, D_CONTENT - BANK + n) for n in range(0, D_MODEL - D_CONTENT, GROUP)),
+)
 EPS = 1e-3
+PIECE = 512
+VCOLS = (512, 512, 512, 512, 512, 512, 1024, 1024)
 TINY = 1e-30
 VECTOR_COLS = 512
-SHARED_TILES = 6
+SHARED_TILES = 7
 LAST_SHARED_COLS = 768
 
 FLOPS = 2 * TOKENS * (HEADS * HALF) * D_MODEL
@@ -52,30 +61,18 @@ def tile_multiheadattention_pa_kernel(
         ab_psum = stack.enter_context(tc.psum_pool(name="ab_psum", bufs=1))
         stack.enter_context(tc.manual_schedule())
 
-        w_both = const.tile([P, PASSES, 2 * D_MODEL], U8, align_bytes=64)
-        w_scales = const.tile([P, PASSES, D_MODEL], U8, align_bytes=64)
+        w_tiles = [const.tile([P, PASSES, 2 * n], U8, align_bytes=64, name="w%d" % n) for n in WIDTHS]
+        s_tiles = [const.tile([P, PASSES, n], U8, align_bytes=64, name="s%d" % n) for n in WIDTHS]
         ab_rows = const.tile([P, BANK], BF16)
         one = const.tile([P, 1], F32)
-        words_sb = w_both[:].bitcast(I32)
-        scales_sb = w_scales[:].bitcast(I32)
-        split_w = D_CONTENT // 2
-        split_s = D_CONTENT // 4
-        nc.vector.memset(ab_rows[:].bitcast(F32), 0.0)
+        nc.vector.memset(w_tiles[0][:].bitcast(I32), 0)
+        nc.vector.memset(s_tiles[0][:].bitcast(I32), 0)
+        nc.vector.memset(s_tiles[1][:].bitcast(I32), 0)
         nc.vector.memset(one[:], 1.0)
-        nc.vector.memset(words_sb[:, :, 0:split_w], 0)
-        nc.vector.memset(scales_sb, 0)
         ident = const.tile([P, P], F32)
+        nc.gpsimd.memset(ab_rows[:].bitcast(F32), 0.0)
         make_identity(nc, ident[:])
-        nc.gpsimd.memset(words_sb[:, :, split_w:], 0)
-
-        for v, vec in enumerate((ln_a, ln_b)):
-            nc.scalar.dma_start(
-                out=ab_rows[BANKS_PER_ROW * v : BANKS_PER_ROW * (v + 1), :],
-                in_=vec.rearrange("(c n) -> c n", c=BANKS_PER_ROW),
-            )
-
-        warm = const.tile([P, 1], F32)
-        nc.scalar.activation(out=warm[:], in_=one[:], func=ACT.Abs_reciprocal_sqrt)
+        nc.gpsimd.memset(w_tiles[1][:].bitcast(I32), 0)
 
         x_src = attn_out.rearrange("h b l f -> h (b l) f")
         x_tiles = []
@@ -91,30 +88,37 @@ def tile_multiheadattention_pa_kernel(
             queue.dma_start(out=inp_tile[:], in_=inp[P * i : P * (i + 1), :])
             inp_tiles.append(inp_tile)
 
-        def load_weights():
-            w1 = w_proj1_words[0].bitcast(I32).rearrange("(g h q) w -> h q g w", g=PASSES, h=HEADS_PER_PASS)
-            w2 = w_proj2_words[0].bitcast(I32).rearrange("(g h q) w -> h q g w", g=PASSES, h=HEADS_PER_PASS)
-            s1 = w_proj1_scales[0].bitcast(I32).rearrange("(g h e) w -> e h g w", g=PASSES, h=HEADS_PER_PASS)
-            s2 = w_proj2_scales[0].bitcast(I32).rearrange("(g h e) w -> e h g w", g=PASSES, h=HEADS_PER_PASS)
-            for h in range(HEADS_PER_PASS):
-                first = 2 * ROWS_PER_HALF * h
-                nc.sync.dma_start(out=words_sb[first : first + ROWS_PER_HALF, :, 0:split_w], in_=w1[h])
+        def load_scales(j, scales):
+            scales_hbm = scales[0].bitcast(I32).rearrange("(g h e) w -> e h g w", g=PASSES, h=HEADS_PER_PASS)
             for e in range(2):
-                nc.sync.dma_start(out=scales_sb[e : P : 32, :, 0:split_s], in_=s1[e])
-            load_x(1, nc.sync)
+                nc.sync.dma_start(out=s_tiles[j][2 * j + e : P : 32, :, :].bitcast(I32), in_=scales_hbm[e])
+
+        def load_words(j, words):
+            words_hbm = words[0].bitcast(I32).rearrange("(g h q) w -> h q g w", g=PASSES, h=HEADS_PER_PASS)
             for h in range(HEADS_PER_PASS):
-                first = 2 * ROWS_PER_HALF * h + ROWS_PER_HALF
-                nc.sync.dma_start(out=words_sb[first : first + ROWS_PER_HALF, :, split_w:], in_=w2[h])
-            for e in range(2):
-                nc.sync.dma_start(out=scales_sb[2 + e : P : 32, :, split_s:], in_=s2[e])
+                first = ROWS_PER_HALF * (2 * h + j)
+                nc.sync.dma_start(
+                    out=w_tiles[j][first : first + ROWS_PER_HALF, :, :].bitcast(I32), in_=words_hbm[h]
+                )
 
         load_x(0, nc.sync)
         load_inp(0, nc.gpsimd)
-        load_weights()
-        for i in range(1, N_TILES):
-            if i + 1 < N_TILES:
-                load_x(i + 1, nc.sync)
-            load_inp(i, nc.sync)
+        for v, vec in enumerate((ln_a, ln_b)):
+            nc.gpsimd.dma_start(
+                out=ab_rows[BANKS_PER_ROW * v : BANKS_PER_ROW * (v + 1), :],
+                in_=vec.rearrange("(c n) -> c n", c=BANKS_PER_ROW),
+            )
+        load_words(0, w_proj1_words)
+        load_scales(0, w_proj1_scales)
+        load_x(1, nc.sync)
+        load_scales(1, w_proj2_scales)
+        load_words(1, w_proj2_words)
+        for i in range(2, N_TILES):
+            load_x(i, nc.sync)
+            load_inp(i - 1, nc.sync)
+        load_inp(N_TILES - 1, nc.sync)
+        warm = const.tile([P, 1], F32)
+        nc.scalar.activation(out=warm[:], in_=one[:], func=ACT.Abs_reciprocal_sqrt)
 
         xt_banks = {}
         grouped_tiles = {}
@@ -163,16 +167,17 @@ def tile_multiheadattention_pa_kernel(
         def project_half(i, c):
             codes, code_scales = code_tiles[i]
             z = z_psum.tile([P, BANK], F32, tag="z%d" % c)
-            for g in range(PASSES):
-                nc.tensor.matmul_mx(
-                    out=z[:],
-                    lhsT=codes[:, P * g : P * (g + 1)].bitcast(FP8X4),
-                    lhsT_scale=code_scales[:, P * g : P * (g + 1)],
-                    rhs=w_both[:, g, 2 * BANK * c : 2 * BANK * (c + 1)].bitcast(FP4X4),
-                    rhs_scale=w_scales[:, g, BANK * c : BANK * (c + 1)],
-                    start=(g == 0),
-                    stop=(g == PASSES - 1),
-                )
+            for j, first, width, at in COLUMN_GROUPS[c]:
+                for g in range(PASSES):
+                    nc.tensor.matmul_mx(
+                        out=z[:, at : at + width],
+                        lhsT=codes[:, P * g : P * (g + 1)].bitcast(FP8X4),
+                        lhsT_scale=code_scales[:, P * g : P * (g + 1)],
+                        rhs=w_tiles[j][:, g, 2 * first : 2 * (first + width)].bitcast(FP4X4),
+                        rhs_scale=s_tiles[j][:, g, first : first + width],
+                        start=(g == 0),
+                        stop=(g == PASSES - 1),
+                    )
             z_banks[(i, c)] = z
 
         def add_residual(i, c):
@@ -231,12 +236,10 @@ def tile_multiheadattention_pa_kernel(
                 small[i]["rstd"] = rstd
 
         def shared(i):
-            return i < SHARED_TILES
+            return VCOLS[i] < D_MODEL
 
         def vector_cols(i):
-            if i == SHARED_TILES - 1:
-                return LAST_SHARED_COLS
-            return VECTOR_COLS if shared(i) else D_MODEL
+            return VCOLS[i]
 
         def vector_pieces(i):
             widths = [min(BANK, vector_cols(i) - BANK * c) for c in range(BANKS_PER_ROW)]
@@ -280,9 +283,11 @@ def tile_multiheadattention_pa_kernel(
             )
 
         def gpsimd_gain_bias(i):
-            rest = o_rows[i][:, vector_cols(i) :]
-            nc.gpsimd.tensor_tensor(out=rest, in0=rest, in1=ab_high[:, 0, vector_cols(i) - VECTOR_COLS :], op=ALU.mult)
-            nc.gpsimd.tensor_tensor(out=rest, in0=rest, in1=ab_high[:, 1, vector_cols(i) - VECTOR_COLS :], op=ALU.add)
+            pieces = [slice(c, min(c + PIECE, D_MODEL)) for c in range(vector_cols(i), D_MODEL, PIECE)]
+            for v, op in ((0, ALU.mult), (1, ALU.add)):
+                for cols in pieces:
+                    part = o_rows[i][:, cols]
+                    nc.gpsimd.tensor_tensor(out=part, in0=part, in1=ab_sbuf[:, v, cols], op=op)
 
         def store_piece(i, first, width):
             nc.sync.dma_start(
@@ -306,64 +311,114 @@ def tile_multiheadattention_pa_kernel(
         transpose_only(0)
         copy_out(0)
         quantise_tile(0)
-        ab_high = const.tile([P, 2, D_MODEL - VECTOR_COLS], BF16)
-        for v in range(2):
-            spread(v, 1)
-            nc.scalar.copy(out=ab_high[:, v, :], in_=ab_banks[(v, 1)][:])
-        project_half(0, 0)
+        ab_sbuf = const.tile([P, 2, D_MODEL], BF16)
         transpose_only(1)
         copy_out(1)
+        project_half(0, 0)
         project_half(0, 1)
-        for v in range(2):
-            spread(v, 0)
 
         def tile_is(i):
             return 0 <= i < N_TILES
 
-        for r in range(N_TILES + 2):
-            if tile_is(r):
-                o_row = results.tile([P, D_MODEL], F32)
-                o_rows[r] = o_row
-                add_residual(r, 0)
+        for r in range(N_TILES + 3):
             if r == 0:
-                add_residual(r, 1)
-            if tile_is(r + 1):
-                quantise_tile(r + 1)
-                project_half(r + 1, 0)
-            if r == 0:
+                if tile_is(r):
+                    o_row = results.tile([P, D_MODEL], F32)
+                    o_rows[r] = o_row
+                    add_residual(r, 0)
+                if tile_is(r + 1):
+                    quantise_tile(r + 1)
+                if tile_is(r):
+                    add_residual(r, 1)
+                if tile_is(r + 1):
+                    project_half(r + 1, 0)
                 transpose_only(2)
-            elif tile_is(r + 3):
-                transpose_only(r + 3)
-            if tile_is(r - 1):
-                vector_gain(r - 1)
-            if tile_is(r) and r > 0:
-                add_residual(r, 1)
-            if tile_is(r + 1):
-                project_half(r + 1, 1)
-            if r == 0:
+                for c in (1, 0):
+                    spread(0, c)
+                if tile_is(r + 1):
+                    project_half(r + 1, 1)
+                for c in (1, 0):
+                    spread(1, c)
                 transpose_only(3)
-            if tile_is(r - 2):
-                vector_bias(r - 2)
-            if tile_is(r - 3) and shared(r - 3):
-                store_piece(r - 3, vector_cols(r - 3), D_MODEL - vector_cols(r - 3))
-            if tile_is(r):
-                negative_mean(r)
-            if tile_is(r - 1):
-                deviation_step(r - 1, 2)
-            if tile_is(r):
-                sum_of_squares(r)
-            if tile_is(r - 1) and shared(r - 1):
-                normalise_shift(r - 1)
-            if r == 0:
+                if tile_is(r):
+                    negative_mean(r)
+                if tile_is(r):
+                    sum_of_squares(r)
                 copy_out(2)
-            elif tile_is(r + 3):
-                copy_out(r + 3)
-            if tile_is(r):
-                deviation_step(r, 0)
-            if r == 0:
+                if tile_is(r):
+                    deviation_step(r, 0)
+                if tile_is(r):
+                    deviation_step(r, 1)
+                if tile_is(r):
+                    deviation_step(r, 2)
+                normalise_shift(r)
+                scalar_normalise(r)
                 copy_out(3)
-            if tile_is(r - 1) and shared(r - 1):
-                scalar_normalise(r - 1)
+            elif r == 1:
+                if tile_is(r):
+                    o_row = results.tile([P, D_MODEL], F32)
+                    o_rows[r] = o_row
+                    add_residual(r, 0)
+                nc.vector.tensor_copy(out=ab_sbuf[:, 0, BANK:], in_=ab_banks[(0, 1)][:])
+                if tile_is(r - 1):
+                    vector_gain(r - 1)
+                if tile_is(r + 1):
+                    quantise_tile(r + 1)
+                if tile_is(r):
+                    add_residual(r, 1)
+                nc.vector.tensor_copy(out=ab_sbuf[:, 1, BANK:], in_=ab_banks[(1, 1)][:])
                 gpsimd_gain_bias(r - 1)
-            if tile_is(r):
-                deviation_step(r, 1)
+                if tile_is(r + 1):
+                    project_half(r + 1, 0)
+                if tile_is(r + 3):
+                    transpose_only(r + 3)
+                if tile_is(r + 1):
+                    project_half(r + 1, 1)
+                if tile_is(r):
+                    negative_mean(r)
+                if tile_is(r):
+                    sum_of_squares(r)
+                if tile_is(r + 3):
+                    copy_out(r + 3)
+                if tile_is(r):
+                    deviation_step(r, 0)
+                if tile_is(r):
+                    deviation_step(r, 1)
+            else:
+                if tile_is(r):
+                    o_row = results.tile([P, D_MODEL], F32)
+                    o_rows[r] = o_row
+                    add_residual(r, 0)
+                if tile_is(r + 1):
+                    quantise_tile(r + 1)
+                if tile_is(r - 1):
+                    vector_gain(r - 1)
+                if tile_is(r):
+                    add_residual(r, 1)
+                if tile_is(r - 2):
+                    vector_bias(r - 2)
+                if tile_is(r + 1):
+                    project_half(r + 1, 0)
+                if tile_is(r + 3):
+                    transpose_only(r + 3)
+                if tile_is(r + 1):
+                    project_half(r + 1, 1)
+                if tile_is(r - 3) and shared(r - 3):
+                    store_piece(r - 3, vector_cols(r - 3), D_MODEL - vector_cols(r - 3))
+                if tile_is(r):
+                    negative_mean(r)
+                if tile_is(r - 1):
+                    deviation_step(r - 1, 2)
+                if tile_is(r):
+                    sum_of_squares(r)
+                if tile_is(r - 1) and shared(r - 1):
+                    normalise_shift(r - 1)
+                if tile_is(r + 3):
+                    copy_out(r + 3)
+                if tile_is(r):
+                    deviation_step(r, 0)
+                if tile_is(r - 1) and shared(r - 1):
+                    scalar_normalise(r - 1)
+                    gpsimd_gain_bias(r - 1)
+                if tile_is(r):
+                    deviation_step(r, 1)

@@ -36,6 +36,7 @@ COLUMN_GROUPS = (
 )
 EPS = 1e-3
 PIECE = 512
+ROWS = 32
 VCOLS = (512, 512, 512, 512, 512, 512, 1024, 1024)
 TINY = 1e-30
 VECTOR_COLS = 512
@@ -63,16 +64,18 @@ def tile_multiheadattention_pa_kernel(
 
         w_tiles = [const.tile([P, PASSES, 2 * n], U8, align_bytes=64, name="w%d" % n) for n in WIDTHS]
         s_tiles = [const.tile([P, PASSES, n], U8, align_bytes=64, name="s%d" % n) for n in WIDTHS]
-        ab_rows = const.tile([P, BANK], BF16)
+        ab_rows = [const.tile([P, BANK], BF16, name="ab_rows%d" % v) for v in range(2)]
         one = const.tile([P, 1], F32)
         nc.vector.memset(w_tiles[0][:].bitcast(I32), 0)
         nc.vector.memset(s_tiles[0][:].bitcast(I32), 0)
         nc.vector.memset(s_tiles[1][:].bitcast(I32), 0)
+        for v in range(2):
+            nc.vector.memset(ab_rows[v][ROWS:64, :].bitcast(F32), 0.0)
+            nc.vector.memset(ab_rows[v][64:P, :].bitcast(F32), 0.0)
         nc.vector.memset(one[:], 1.0)
         ident = const.tile([P, P], F32)
-        nc.gpsimd.memset(ab_rows[:].bitcast(F32), 0.0)
-        make_identity(nc, ident[:])
         nc.gpsimd.memset(w_tiles[1][:].bitcast(I32), 0)
+        make_identity(nc, ident[:])
 
         x_src = attn_out.rearrange("h b l f -> h (b l) f")
         x_tiles = []
@@ -101,13 +104,13 @@ def tile_multiheadattention_pa_kernel(
                     out=w_tiles[j][first : first + ROWS_PER_HALF, :, :].bitcast(I32), in_=words_hbm[h]
                 )
 
+        for v, vec in enumerate((ln_a, ln_b)):
+            halves = vec.rearrange("(c n) -> c n", c=BANKS_PER_ROW)
+            nc.sync.dma_start(
+                out=ab_rows[v][0:ROWS, :], in_=halves.unsqueeze(0).to_broadcast([ROWS // BANKS_PER_ROW, BANKS_PER_ROW, BANK])
+            )
         load_x(0, nc.sync)
         load_inp(0, nc.gpsimd)
-        for v, vec in enumerate((ln_a, ln_b)):
-            nc.gpsimd.dma_start(
-                out=ab_rows[BANKS_PER_ROW * v : BANKS_PER_ROW * (v + 1), :],
-                in_=vec.rearrange("(c n) -> c n", c=BANKS_PER_ROW),
-            )
         load_words(0, w_proj1_words)
         load_scales(0, w_proj1_scales)
         load_x(1, nc.sync)
@@ -287,7 +290,7 @@ def tile_multiheadattention_pa_kernel(
             for v, op in ((0, ALU.mult), (1, ALU.add)):
                 for cols in pieces:
                     part = o_rows[i][:, cols]
-                    nc.gpsimd.tensor_tensor(out=part, in0=part, in1=ab_sbuf[:, v, cols], op=op)
+                    nc.gpsimd.tensor_tensor(out=part, in0=part, in1=ab_high[:, v, cols.start - BANK : cols.stop - BANK], op=op)
 
         def store_piece(i, first, width):
             nc.sync.dma_start(
@@ -297,24 +300,28 @@ def tile_multiheadattention_pa_kernel(
         ident_bf = ident[:].bitcast(BF16)
 
         def spread(v, c):
-            row = BANKS_PER_ROW * v + c
             bank = ab_psum.tile([P, BANK], F32, tag="ab%d%d" % (v, c))
             nc.tensor.matmul(
                 bank[:],
-                lhsT=ident_bf[:, 2 * row + 1 : 2 * row + 2].to_broadcast([P, P]),
-                rhs=ab_rows[:],
+                lhsT=ident_bf[:, 2 * c + 1 : 2 * c + 2].to_broadcast([P, P]),
+                rhs=ab_rows[v][:],
                 start=True,
                 stop=True,
             )
             ab_banks[(v, c)] = bank
 
+        ab_high = const.tile([P, 2, D_MODEL - BANK], BF16)
+        for v in range(2):
+            spread(v, 1)
+            nc.vector.tensor_copy(out=ab_high[:, v, :], in_=ab_banks[(v, 1)][:])
         transpose_only(0)
         copy_out(0)
         quantise_tile(0)
-        ab_sbuf = const.tile([P, 2, D_MODEL], BF16)
+        for v in range(2):
+            spread(v, 0)
+        project_half(0, 0)
         transpose_only(1)
         copy_out(1)
-        project_half(0, 0)
         project_half(0, 1)
 
         def tile_is(i):
@@ -326,19 +333,15 @@ def tile_multiheadattention_pa_kernel(
                     o_row = results.tile([P, D_MODEL], F32)
                     o_rows[r] = o_row
                     add_residual(r, 0)
-                if tile_is(r + 1):
-                    quantise_tile(r + 1)
                 if tile_is(r):
                     add_residual(r, 1)
                 if tile_is(r + 1):
+                    quantise_tile(r + 1)
+                if tile_is(r + 1):
                     project_half(r + 1, 0)
                 transpose_only(2)
-                for c in (1, 0):
-                    spread(0, c)
                 if tile_is(r + 1):
                     project_half(r + 1, 1)
-                for c in (1, 0):
-                    spread(1, c)
                 transpose_only(3)
                 if tile_is(r):
                     negative_mean(r)
@@ -347,27 +350,20 @@ def tile_multiheadattention_pa_kernel(
                 copy_out(2)
                 if tile_is(r):
                     deviation_step(r, 0)
+                copy_out(3)
                 if tile_is(r):
                     deviation_step(r, 1)
-                if tile_is(r):
-                    deviation_step(r, 2)
-                normalise_shift(r)
-                scalar_normalise(r)
-                copy_out(3)
             elif r == 1:
                 if tile_is(r):
                     o_row = results.tile([P, D_MODEL], F32)
                     o_rows[r] = o_row
                     add_residual(r, 0)
-                nc.vector.tensor_copy(out=ab_sbuf[:, 0, BANK:], in_=ab_banks[(0, 1)][:])
                 if tile_is(r - 1):
                     vector_gain(r - 1)
                 if tile_is(r + 1):
                     quantise_tile(r + 1)
                 if tile_is(r):
                     add_residual(r, 1)
-                nc.vector.tensor_copy(out=ab_sbuf[:, 1, BANK:], in_=ab_banks[(1, 1)][:])
-                gpsimd_gain_bias(r - 1)
                 if tile_is(r + 1):
                     project_half(r + 1, 0)
                 if tile_is(r + 3):
@@ -376,12 +372,19 @@ def tile_multiheadattention_pa_kernel(
                     project_half(r + 1, 1)
                 if tile_is(r):
                     negative_mean(r)
+                if tile_is(r - 1):
+                    deviation_step(r - 1, 2)
                 if tile_is(r):
                     sum_of_squares(r)
+                if tile_is(r - 1) and shared(r - 1):
+                    normalise_shift(r - 1)
                 if tile_is(r + 3):
                     copy_out(r + 3)
                 if tile_is(r):
                     deviation_step(r, 0)
+                if tile_is(r - 1) and shared(r - 1):
+                    scalar_normalise(r - 1)
+                    gpsimd_gain_bias(r - 1)
                 if tile_is(r):
                     deviation_step(r, 1)
             else:

@@ -110,10 +110,10 @@ def tile_multiheadattention_pa_kernel(
                 out=ab_rows[v][0:ROWS, :], in_=halves.unsqueeze(0).to_broadcast([ROWS // BANKS_PER_ROW, BANKS_PER_ROW, BANK])
             )
         load_x(0, nc.sync)
-        load_inp(0, nc.gpsimd)
         load_words(0, w_proj1_words)
         load_scales(0, w_proj1_scales)
         load_x(1, nc.sync)
+        load_inp(0, nc.sync)
         load_scales(1, w_proj2_scales)
         load_words(1, w_proj2_words)
         for i in range(2, N_TILES):

from contextlib import ExitStack

import concourse.mybir as mybir
from concourse.masks import make_identity

F32 = mybir.dt.float32
BF16 = mybir.dt.bfloat16
I32 = mybir.dt.int32
U32 = mybir.dt.uint32
U8 = mybir.dt.uint8
FP8X4 = mybir.dt.float8_e4m3fn_x4
FP4X4 = mybir.dt.float4_e2m1fn_x4
ALU = mybir.AluOpType
ACT = mybir.ActivationFunctionType

P = 128
PACK = 4
HEADS = 8
D_V = 128
HALF = D_V // 2
TOKENS = 1024
D_MODEL = 1024
D_CONTENT = 768
N_TILES = TOKENS // P
PASSES = HEADS * D_V // (P * PACK)
HEADS_PER_PASS = HEADS // PASSES
ROWS_PER_HALF = HALF // PACK
BANK = 512
BANKS_PER_ROW = D_MODEL // BANK
WIDTHS = (D_CONTENT, D_MODEL - D_CONTENT)
GROUP = 128
COLUMN_GROUPS = (
    ((0, 0, BANK, 0),),
    tuple((0, BANK + n, GROUP, n) for n in range(0, D_CONTENT - BANK, GROUP))
    + tuple((1, n, GROUP, D_CONTENT - BANK + n) for n in range(0, D_MODEL - D_CONTENT, GROUP)),
)
EPS = 1e-3
PIECE = 512
ROWS = 32
VCOLS = (512, 512, 512, 512, 512, 512, 1024, 1024)
TINY = 1e-30
VECTOR_COLS = 512
SHARED_TILES = 7
LAST_SHARED_COLS = 768

FLOPS = 2 * TOKENS * (HEADS * HALF) * D_MODEL


def tile_multiheadattention_pa_kernel(
    tc, attn_out, inp, w_proj1_words, w_proj1_scales, w_proj2_words, w_proj2_scales, ln_a, ln_b, out
):
    nc = tc.nc
    with ExitStack() as stack:
        const = stack.enter_context(tc.tile_pool(name="const", bufs=1))
        loads = stack.enter_context(tc.tile_pool(name="loads", bufs=N_TILES))
        stage = stack.enter_context(tc.tile_pool(name="stage", bufs=4))
        rows = stack.enter_context(tc.tile_pool(name="rows", bufs=4))
        results = stack.enter_context(tc.tile_pool(name="results", bufs=N_TILES))
        stats = stack.enter_context(tc.tile_pool(name="stats", bufs=4))
        xt_psum = stack.enter_context(tc.psum_pool(name="xt_psum", bufs=2))
        z_psum = stack.enter_context(tc.psum_pool(name="z_psum", bufs=1))
        ab_psum = stack.enter_context(tc.psum_pool(name="ab_psum", bufs=1))
        stack.enter_context(tc.manual_schedule())

        w_tiles = [const.tile([P, PASSES, 2 * n], U8, align_bytes=64, name="w%d" % n) for n in WIDTHS]
        s_tiles = [const.tile([P, PASSES, n], U8, align_bytes=64, name="s%d" % n) for n in WIDTHS]
        ab_rows = [const.tile([P, BANK], BF16, name="ab_rows%d" % v) for v in range(2)]
        one = const.tile([P, 1], F32)
        nc.vector.memset(w_tiles[0][:].bitcast(I32), 0)
        nc.vector.memset(s_tiles[0][:].bitcast(I32), 0)
        nc.vector.memset(s_tiles[1][:].bitcast(I32), 0)
        for v in range(2):
            nc.vector.memset(ab_rows[v][ROWS:64, :].bitcast(F32), 0.0)
            nc.vector.memset(ab_rows[v][64:P, :].bitcast(F32), 0.0)
        nc.vector.memset(one[:], 1.0)
        ident = const.tile([P, P], F32)
        nc.gpsimd.memset(w_tiles[1][:].bitcast(I32), 0)
        make_identity(nc, ident[:])

        x_src = attn_out.rearrange("h b l f -> h (b l) f")
        x_tiles = []
        inp_tiles = []

        def load_x(i, queue):
            x_tile = loads.tile([P, HEADS, D_V], BF16)
            queue.dma_start(out=x_tile[:], in_=x_src[:, P * i : P * (i + 1), :].rearrange("h p f -> p h f"))
            x_tiles.append(x_tile)

        def load_inp(i, queue):
            inp_tile = loads.tile([P, D_MODEL], BF16)
            queue.dma_start(out=inp_tile[:], in_=inp[P * i : P * (i + 1), :])
            inp_tiles.append(inp_tile)

        def load_scales(j, scales):
            scales_hbm = scales[0].bitcast(I32).rearrange("(g h e) w -> e h g w", g=PASSES, h=HEADS_PER_PASS)
            for e in range(2):
                nc.sync.dma_start(out=s_tiles[j][2 * j + e : P : 32, :, :].bitcast(I32), in_=scales_hbm[e])

        def load_words(j, words):
            words_hbm = words[0].bitcast(I32).rearrange("(g h q) w -> h q g w", g=PASSES, h=HEADS_PER_PASS)
            for h in range(HEADS_PER_PASS):
                first = ROWS_PER_HALF * (2 * h + j)
                nc.sync.dma_start(
                    out=w_tiles[j][first : first + ROWS_PER_HALF, :, :].bitcast(I32), in_=words_hbm[h]
                )

        for v, vec in enumerate((ln_a, ln_b)):
            halves = vec.rearrange("(c n) -> c n", c=BANKS_PER_ROW)
            nc.sync.dma_start(
                out=ab_rows[v][0:ROWS, :], in_=halves.unsqueeze(0).to_broadcast([ROWS // BANKS_PER_ROW, BANKS_PER_ROW, BANK])
            )
        load_x(0, nc.sync)
        load_words(0, w_proj1_words)
        load_scales(0, w_proj1_scales)
        load_x(1, nc.sync)
        load_inp(0, nc.sync)
        load_scales(1, w_proj2_scales)
        load_words(1, w_proj2_words)
        for i in range(2, N_TILES):
            load_x(i, nc.sync)
            load_inp(i - 1, nc.sync)
        load_inp(N_TILES - 1, nc.sync)
        warm = const.tile([P, 1], F32)
        nc.scalar.activation(out=warm[:], in_=one[:], func=ACT.Abs_reciprocal_sqrt)

        xt_banks = {}
        grouped_tiles = {}
        code_tiles = {}
        z_banks = {}
        ab_banks = {}
        z_rows = {}
        o_rows = {}
        small = {}

        def transpose_only(i):
            x_words = x_tiles[i][:].rearrange("p h f -> p (h f)").bitcast(F32)
            words_per_pass = P * PACK // 2
            xt = xt_psum.tile([P, PASSES, 2, P], F32)
            for g in range(PASSES):
                for u in range(2):
                    nc.tensor.transpose(
                        xt[:, g, u, :],
                        x_words[:, words_per_pass * g + u : words_per_pass * (g + 1) : 2],
                        ident[:],
                    )
            xt_banks[i] = xt

        def copy_out(i):
            xt = xt_banks[i]
            grouped = stage.tile([P, PASSES, P, PACK], BF16, align_bytes=64)
            grouped_words = (
                grouped[:]
                .rearrange("p g r t -> p (g r t)")
                .bitcast(F32)
                .rearrange("p (g r u) -> p g r u", g=PASSES, u=2)
            )
            nc.scalar.copy(out=grouped_words, in_=xt[:].rearrange("p g u r -> p g r u"))
            grouped_tiles[i] = grouped

        def quantise_tile(i):
            codes = stage.tile([P, PASSES * P], U32, align_bytes=64)
            code_scales = stage.tile([P, PASSES * P], U8, align_bytes=64)
            nc.vector.quantize_mx(
                out=codes[:].bitcast(FP8X4),
                scales=code_scales[:],
                in_=grouped_tiles[i][:].rearrange("p g r t -> p (g r t)"),
            )
            code_tiles[i] = (codes, code_scales)

        def project_half(i, c):
            codes, code_scales = code_tiles[i]
            z = z_psum.tile([P, BANK], F32, tag="z%d" % c)
            for j, first, width, at in COLUMN_GROUPS[c]:
                for g in range(PASSES):
                    nc.tensor.matmul_mx(
                        out=z[:, at : at + width],
                        lhsT=codes[:, P * g : P * (g + 1)].bitcast(FP8X4),
                        lhsT_scale=code_scales[:, P * g : P * (g + 1)],
                        rhs=w_tiles[j][:, g, 2 * first : 2 * (first + width)].bitcast(FP4X4),
                        rhs_scale=s_tiles[j][:, g, first : first + width],
                        start=(g == 0),
                        stop=(g == PASSES - 1),
                    )
            z_banks[(i, c)] = z

        def add_residual(i, c):
            if c == 0:
                z_row = rows.tile([P, D_MODEL], F32)
                sums = stats.tile([P, BANKS_PER_ROW], F32)
                z_rows[i] = z_row
                small[i] = {"sums": sums}
            cols = slice(BANK * c, BANK * (c + 1))
            nc.vector.scalar_tensor_tensor(
                out=z_rows[i][:, cols],
                in0=z_banks[(i, c)][:],
                scalar=1.0,
                in1=inp_tiles[i][:, cols],
                op0=ALU.mult,
                op1=ALU.add,
                accum_out=small[i]["sums"][:, c : c + 1],
            )

        def negative_mean(i):
            scaled = stats.tile([P, BANKS_PER_ROW], F32)
            neg_mean = stats.tile([P, 1], F32)
            nc.scalar.activation(
                out=scaled[:], in_=small[i]["sums"][:], func=ACT.Identity, scale=-1.0 / D_MODEL, accum_out=neg_mean[:]
            )
            small[i]["neg_mean"] = neg_mean

        def sum_of_squares(i):
            squares = rows.tile([P, D_MODEL], BF16)
            ssq = stats.tile([P, 1], F32)
            nc.scalar.activation(
                out=squares[:], in_=z_rows[i][:], func=ACT.Square, bias=small[i]["neg_mean"][:], accum_out=ssq[:]
            )
            small[i]["ssq"] = ssq

        def deviation_step(i, step):
            if step == 0:
                inv_root = stats.tile([P, 1], F32)
                nc.scalar.activation(
                    out=inv_root[:],
                    in_=small[i]["ssq"][:],
                    func=ACT.Abs_reciprocal_sqrt,
                    scale=float(D_MODEL - 1),
                    bias=TINY,
                )
                small[i]["inv_root"] = inv_root
            if step == 1:
                shifted_sq = stats.tile([P, 1], F32)
                nc.scalar.activation(
                    out=shifted_sq[:], in_=small[i]["ssq"][:], func=ACT.Square, scale=small[i]["inv_root"][:], bias=EPS
                )
                small[i]["shifted_sq"] = shifted_sq
            if step == 2:
                rstd = stats.tile([P, 1], F32)
                nc.scalar.activation(out=rstd[:], in_=small[i]["shifted_sq"][:], func=ACT.Abs_reciprocal_sqrt)
                small[i]["rstd"] = rstd

        def shared(i):
            return VCOLS[i] < D_MODEL

        def vector_cols(i):
            return VCOLS[i]

        def vector_pieces(i):
            widths = [min(BANK, vector_cols(i) - BANK * c) for c in range(BANKS_PER_ROW)]
            return [(BANK * c, widths[c], c) for c in range(BANKS_PER_ROW) if widths[c] > 0]

        def vector_gain(i):
            for first, width, c in vector_pieces(i):
                nc.vector.scalar_tensor_tensor(
                    out=o_rows[i][:, first : first + width],
                    in0=z_rows[i][:, first : first + width],
                    scalar=small[i]["neg_mean"][:],
                    in1=ab_banks[(0, c)][:, 0:width],
                    op0=ALU.add,
                    op1=ALU.mult,
                )

        def vector_bias(i):
            for first, width, c in vector_pieces(i):
                nc.vector.scalar_tensor_tensor(
                    out=o_rows[i][:, first : first + width],
                    in0=o_rows[i][:, first : first + width],
                    scalar=small[i]["rstd"][:],
                    in1=ab_banks[(1, c)][:, 0:width],
                    op0=ALU.mult,
                    op1=ALU.add,
                )
                store_piece(i, first, width)

        def normalise_shift(i):
            shift = stats.tile([P, 1], F32)
            nc.scalar.activation(out=shift[:], in_=small[i]["neg_mean"][:], func=ACT.Copy, scale=small[i]["rstd"][:])
            small[i]["shift"] = shift

        def scalar_normalise(i):
            nc.scalar.activation(
                out=o_rows[i][:, vector_cols(i) :],
                in_=z_rows[i][:, vector_cols(i) :],
                func=ACT.Identity,
                scale=small[i]["rstd"][:],
                bias=small[i]["shift"][:],
            )

        def gpsimd_gain_bias(i):
            pieces = [slice(c, min(c + PIECE, D_MODEL)) for c in range(vector_cols(i), D_MODEL, PIECE)]
            for v, op in ((0, ALU.mult), (1, ALU.add)):
                for cols in pieces:
                    part = o_rows[i][:, cols]
                    nc.gpsimd.tensor_tensor(out=part, in0=part, in1=ab_high[:, v, cols.start - BANK : cols.stop - BANK], op=op)

        def store_piece(i, first, width):
            nc.sync.dma_start(
                out=out[P * i : P * (i + 1), first : first + width], in_=o_rows[i][:, first : first + width]
            )

        ident_bf = ident[:].bitcast(BF16)

        def spread(v, c):
            bank = ab_psum.tile([P, BANK], F32, tag="ab%d%d" % (v, c))
            nc.tensor.matmul(
                bank[:],
                lhsT=ident_bf[:, 2 * c + 1 : 2 * c + 2].to_broadcast([P, P]),
                rhs=ab_rows[v][:],
                start=True,
                stop=True,
            )
            ab_banks[(v, c)] = bank

        ab_high = const.tile([P, 2, D_MODEL - BANK], BF16)
        for v in range(2):
            spread(v, 1)
            nc.vector.tensor_copy(out=ab_high[:, v, :], in_=ab_banks[(v, 1)][:])
        transpose_only(0)
        copy_out(0)
        quantise_tile(0)
        for v in range(2):
            spread(v, 0)
        project_half(0, 0)
        transpose_only(1)
        copy_out(1)
        project_half(0, 1)

        def tile_is(i):
            return 0 <= i < N_TILES

        for r in range(N_TILES + 3):
            if r == 0:
                if tile_is(r):
                    o_row = results.tile([P, D_MODEL], F32)
                    o_rows[r] = o_row
                    add_residual(r, 0)
                if tile_is(r):
                    add_residual(r, 1)
                if tile_is(r + 1):
                    quantise_tile(r + 1)
                if tile_is(r + 1):
                    project_half(r + 1, 0)
                transpose_only(2)
                if tile_is(r + 1):
                    project_half(r + 1, 1)
                transpose_only(3)
                if tile_is(r):
                    negative_mean(r)
                if tile_is(r):
                    sum_of_squares(r)
                copy_out(2)
                if tile_is(r):
                    deviation_step(r, 0)
                copy_out(3)
                if tile_is(r):
                    deviation_step(r, 1)
            elif r == 1:
                if tile_is(r):
                    o_row = results.tile([P, D_MODEL], F32)
                    o_rows[r] = o_row
                    add_residual(r, 0)
                if tile_is(r - 1):
                    vector_gain(r - 1)
                if tile_is(r + 1):
                    quantise_tile(r + 1)
                if tile_is(r):
                    add_residual(r, 1)
                if tile_is(r + 1):
                    project_half(r + 1, 0)
                if tile_is(r + 3):
                    transpose_only(r + 3)
                if tile_is(r + 1):
                    project_half(r + 1, 1)
                if tile_is(r):
                    negative_mean(r)
                if tile_is(r - 1):
                    deviation_step(r - 1, 2)
                if tile_is(r):
                    sum_of_squares(r)
                if tile_is(r - 1) and shared(r - 1):
                    normalise_shift(r - 1)
                if tile_is(r + 3):
                    copy_out(r + 3)
                if tile_is(r):
                    deviation_step(r, 0)
                if tile_is(r - 1) and shared(r - 1):
                    scalar_normalise(r - 1)
                    gpsimd_gain_bias(r - 1)
                if tile_is(r):
                    deviation_step(r, 1)
            else:
                if tile_is(r):
                    o_row = results.tile([P, D_MODEL], F32)
                    o_rows[r] = o_row
                    add_residual(r, 0)
                if tile_is(r + 1):
                    quantise_tile(r + 1)
                if tile_is(r - 1):
                    vector_gain(r - 1)
                if tile_is(r):
                    add_residual(r, 1)
                if tile_is(r - 2):
                    vector_bias(r - 2)
                if tile_is(r + 1):
                    project_half(r + 1, 0)
                if tile_is(r + 3):
                    transpose_only(r + 3)
                if tile_is(r + 1):
                    project_half(r + 1, 1)
                if tile_is(r - 3) and shared(r - 3):
                    store_piece(r - 3, vector_cols(r - 3), D_MODEL - vector_cols(r - 3))
                if tile_is(r):
                    negative_mean(r)
                if tile_is(r - 1):
                    deviation_step(r - 1, 2)
                if tile_is(r):
                    sum_of_squares(r)
                if tile_is(r - 1) and shared(r - 1):
                    normalise_shift(r - 1)
                if tile_is(r + 3):
                    copy_out(r + 3)
                if tile_is(r):
                    deviation_step(r, 0)
                if tile_is(r - 1) and shared(r - 1):
                    scalar_normalise(r - 1)
                    gpsimd_gain_bias(r - 1)
                if tile_is(r):
                    deviation_step(r, 1)
